import numpy as np
import ml_dtypes

BF16 = ml_dtypes.bfloat16


def bf(x):
    return np.asarray(x, np.float32).astype(BF16)


def f32(x):
    return np.asarray(x, np.float32)


def f64(x):
    return np.asarray(x).astype(np.float64)


def striped(idx):
    return np.tile(idx.reshape(-1, 16).T, (8, 1))


S, E, H, D, N = 2048, 128, 128, 4, 1024
SLOPE, EPS = 0.3, 1e-7


def leaky(v):
    return np.maximum(v, SLOPE * v)


def age_grid():
    r = S // N
    q = np.linspace(-1.0, 1.0, D * N)
    return q * np.sqrt((r * q.size - 1.0) / (r * np.sum(q * q)))


def setup_inputs():
    length = 0.5 + np.random.random((S, 1))
    return {
        "table": bf(np.random.standard_normal((S, E)) * length / np.sqrt(E)),
        "w_in": bf(np.random.standard_normal((E, H))),
        "w_age": f32(np.random.standard_normal((H, 1))),
        "b_in": f32(0.1 * np.random.standard_normal((H, 1))),
        "age": f32(np.random.permutation(age_grid()).reshape(D, N)),
        "w_hid": bf(np.random.standard_normal((H, H)) / np.sqrt(H)),
        "b_hid": f32(0.1 * np.random.standard_normal((H, 1))),
        "offs": striped(np.random.permutation(S)[:N]),
    }


def reference(table, w_in, w_age, b_in, age, w_hid, b_hid, offs):
    idx = offs[:16].T.reshape(-1)
    t = f64(table)
    norm = np.sqrt(np.sum(t * t, axis=1, keepdims=True))
    embs = t * np.minimum(1.0, 1.0 / (norm + EPS))
    proj = f64(w_in).T @ embs[idx].T
    z = proj[:, None, :] + f64(w_age)[:, :, None] * np.maximum(f64(age), 0.0)[None, :, :] + f64(b_in)[:, :, None]
    h = leaky(z).reshape(H, D * N)
    return leaky(f64(w_hid).T @ h + f64(b_hid))

@@ -1,0 +1,155 @@
+import concourse.masks as masks
+import concourse.mybir as mybir
+
+S, E, H, D, N = 2048, 128, 128, 4, 1024
+SLOPE, EPS = 0.3, 1e-7
+FLOPS = 2 * E * H * N + 2 * H * H * D * N
+
+P = 128
+BLOCKS = S // P
+HALF = BLOCKS // 2
+PIECE = 512
+PIECES = N // PIECE
+FLIP = PIECE // P
+LAG = 3
+FLT_MAX = 3.4028234663852886e38
+
+BF16, F32, U16 = mybir.dt.bfloat16, mybir.dt.float32, mybir.dt.uint16
+ADD, MULT = mybir.AluOpType.add, mybir.AluOpType.mult
+MAX, MIN = mybir.AluOpType.max, mybir.AluOpType.min
+ACT = mybir.ActivationFunctionType
+
+
+def tile_temporalnmf_kernel(tc, table, w_in, w_age, b_in, age, w_hid, b_hid, offs, out):
+    nc = tc.nc
+    with (
+        tc.tile_pool(name="held", bufs=1) as held,
+        tc.psum_pool(name="proj_banks", bufs=1) as proj_banks,
+    ):
+        table_blocks = table.rearrange("(b p) e -> p b e", p=P)
+        rows = held.tile([P, BLOCKS, E], BF16, name="rows")
+        for quarter in range(4):
+            blocks = slice(quarter * FLIP, (quarter + 1) * FLIP)
+            queue = nc.sync if quarter % 2 == 0 else nc.scalar
+            queue.dma_start(rows[:, blocks, :], table_blocks[:, blocks, :])
+        offsets = held.tile([P, N // 16], U16, name="offsets")
+        nc.sync.dma_start(offsets[:], offs)
+
+        b_in_row = held.tile([1, H], F32, name="b_in_row")
+        nc.sync.dma_start(b_in_row[:], b_in.rearrange("k one -> one k"))
+        w_in_sb = held.tile([E, H], BF16, name="w_in_sb")
+        nc.scalar.dma_start(w_in_sb[:], w_in)
+        w_hid_sb = held.tile([H, H], BF16, name="w_hid_sb")
+        nc.scalar.dma_start(w_hid_sb[:], w_hid)
+        w_age_col = held.tile([H, 1], F32, name="w_age_col")
+        nc.sync.dma_start(w_age_col[:], w_age)
+        b_hid_col = held.tile([H, 1], F32, name="b_hid_col")
+        nc.scalar.dma_start(b_hid_col[:], b_hid)
+        ages = [held.tile([P, N], F32, name=f"ages{t}") for t in range(D)]
+        for t in range(D):
+            queue = nc.sync if t % 2 == 0 else nc.scalar
+            queue.dma_start(ages[t][:], age[t, :].partition_broadcast(P))
+
+        dummy = held.tile([P, 1], F32, name="dummy")
+        nc.gpsimd.memset(dummy[:], 1.0)
+        nc.scalar.sqrt(dummy[:], dummy[:])
+        identity = held.tile([P, P], BF16, name="identity")
+        masks.make_identity(nc, identity[:])
+        ones_row = held.tile([1, PIECE], F32, name="ones_row")
+        nc.gpsimd.memset(ones_row[:], 1.0)
+
+        proj = [proj_banks.tile([H, PIECE], F32, name=f"proj{g}") for g in range(PIECES)]
+        for g in range(PIECES):
+            nc.tensor.matmul(proj[g][:], b_in_row[:], ones_row[:], start=True, stop=False)
+
+        w_hid_minus = held.tile([H, H], BF16, name="w_hid_minus")
+        nc.gpsimd.tensor_scalar_mul(w_hid_minus[:], w_hid_sb[:], -1.0)
+        b_hid_low = held.tile([H, 1], F32, name="b_hid_low")
+        nc.gpsimd.tensor_scalar_mul(b_hid_low[:], b_hid_col[:], SLOPE)
+        for t in range(D):
+            nc.gpsimd.tensor_scalar(ages[t][:], ages[t][:], FLT_MAX, 0.0, op0=MIN, op1=MAX)
+
+        window = held.tile([E, S], BF16, name="window")
+        with (
+            tc.tile_pool(name="shrinking", bufs=1) as shrinking,
+            tc.psum_pool(name="flip_banks", bufs=1) as flip_banks,
+        ):
+            squares = shrinking.tile([P, BLOCKS, E], F32, name="squares")
+            sumsq = shrinking.tile([P, BLOCKS], F32, name="sumsq")
+            for quarter in range(2):
+                blocks = slice(quarter * FLIP, (quarter + 1) * FLIP)
+                nc.vector.tensor_tensor(squares[:, blocks, :], rows[:, blocks, :], rows[:, blocks, :], MULT)
+                nc.vector.reduce_sum(sumsq[:, blocks], squares[:, blocks, :], axis=mybir.AxisListType.X)
+            for b in range(HALF, BLOCKS):
+                nc.scalar.activation(squares[:, b, :], rows[:, b, :], ACT.Square, accum_out=sumsq[:, b : b + 1])
+
+            norm = shrinking.tile([P, BLOCKS], F32, name="norm")
+            nc.scalar.sqrt(norm[:], sumsq[:])
+            divisor = shrinking.tile([P, BLOCKS], F32, name="divisor")
+            nc.vector.tensor_scalar(divisor[:], norm[:], EPS, 1.0, op0=ADD, op1=MAX)
+            factor = shrinking.tile([P, BLOCKS], F32, name="factor")
+            nc.vector.reciprocal(factor[:], divisor[:])
+
+            embs_rows = shrinking.tile([P, BLOCKS, E], BF16, name="embs_rows")
+            flipped = [flip_banks.tile([E, PIECE], BF16, name=f"flipped{q}") for q in range(BLOCKS // FLIP)]
+            for i in range(HALF):
+                for b in (i, HALF + i):
+                    if b < HALF:
+                        nc.vector.tensor_scalar(embs_rows[:, b, :], rows[:, b, :], factor[:, b : b + 1], None, op0=MULT)
+                    else:
+                        nc.scalar.activation(embs_rows[:, b, :], rows[:, b, :], ACT.Copy, scale=factor[:, b : b + 1])
+                    nc.tensor.transpose(
+                        flipped[b // FLIP][:, (b % FLIP) * P : (b % FLIP + 1) * P], embs_rows[:, b, :], identity[:]
+                    )
+            for q in (0, 2, 1, 3):
+                columns = slice(q * PIECE, (q + 1) * PIECE)
+                if q * FLIP < HALF:
+                    nc.vector.tensor_copy(window[:, columns], flipped[q][:])
+                else:
+                    nc.scalar.copy(window[:, columns], flipped[q][:])
+
+        for g in range(PIECES):
+            piece = offsets[:, g * (PIECE // 16) : (g + 1) * (PIECE // 16)]
+            nc.tensor.matmul(proj[g][:], w_in_sb[:], window[:].indirect(piece), start=False, stop=True)
+
+        with (
+            tc.tile_pool(name="work", bufs=4) as work,
+            tc.psum_pool(name="y_banks", bufs=LAG + 2) as y_banks,
+        ):
+            chunks = [(t, g) for t in range(D) for g in range(PIECES)]
+            products = []
+
+            def first_layer(t, g):
+                z = work.tile([H, PIECE], F32, name="z")
+                nc.vector.scalar_tensor_tensor(
+                    out=z[:],
+                    in0=ages[t][:, g * PIECE : (g + 1) * PIECE],
+                    scalar=w_age_col[:, 0:1],
+                    in1=proj[g][:],
+                    op0=MULT,
+                    op1=ADD,
+                )
+                h_plus = work.tile([H, PIECE], BF16, name="h_plus")
+                nc.gpsimd.tensor_scalar(h_plus[:], z[:], FLT_MAX, 0.0, op0=MIN, op1=MAX)
+                h_minus = work.tile([H, PIECE], BF16, name="h_minus")
+                nc.scalar.activation(h_minus[:], z[:], ACT.Relu, scale=-SLOPE)
+                y = y_banks.tile([H, PIECE], F32, name="y")
+                nc.tensor.matmul(y[:], w_hid_sb[:], h_plus[:], start=True, stop=False)
+                nc.tensor.matmul(y[:], w_hid_minus[:], h_minus[:], start=False, stop=True)
+                products.append(y)
+
+            def second_layer(c):
+                y = products[c]
+                low = work.tile([H, PIECE], F32, name="low")
+                nc.scalar.activation(low[:], y[:], ACT.Identity, bias=b_hid_low[:, 0:1], scale=SLOPE)
+                result = work.tile([H, PIECE], F32, name="result")
+                nc.vector.scalar_tensor_tensor(
+                    out=result[:], in0=y[:], scalar=b_hid_col[:, 0:1], in1=low[:], op0=ADD, op1=MAX
+                )
+                nc.sync.dma_start(out[:, c * PIECE : (c + 1) * PIECE], result[:])
+
+            for step in range(len(chunks) + LAG):
+                if step < len(chunks):
+                    first_layer(*chunks[step])
+                if step >= LAG:
+                    second_layer(step - LAG)

@@ -12,11 +12,10 @@ PIECE = 512
 PIECES = N // PIECE
 FLIP = PIECE // P
 LAG = 3
-FLT_MAX = 3.4028234663852886e38
 
 BF16, F32, U16 = mybir.dt.bfloat16, mybir.dt.float32, mybir.dt.uint16
 ADD, MULT = mybir.AluOpType.add, mybir.AluOpType.mult
-MAX, MIN = mybir.AluOpType.max, mybir.AluOpType.min
+MAX = mybir.AluOpType.max
 ACT = mybir.ActivationFunctionType
 
 
@@ -26,48 +25,37 @@ def tile_temporalnmf_kernel(tc, table, w_in, w_age, b_in, age, w_hid, b_hid, off
         tc.tile_pool(name="held", bufs=1) as held,
         tc.psum_pool(name="proj_banks", bufs=1) as proj_banks,
     ):
-        table_blocks = table.rearrange("(b p) e -> p b e", p=P)
+        table_quarters = table.rearrange("(q p i) e -> q p i e", p=P, i=FLIP)
         rows = held.tile([P, BLOCKS, E], BF16, name="rows")
-        for quarter in range(4):
-            blocks = slice(quarter * FLIP, (quarter + 1) * FLIP)
-            queue = nc.sync if quarter % 2 == 0 else nc.scalar
-            queue.dma_start(rows[:, blocks, :], table_blocks[:, blocks, :])
+        for q in (0, 2, 1, 3):
+            queue = nc.sync if q * FLIP < HALF else nc.scalar
+            queue.dma_start(rows[:, q * FLIP : (q + 1) * FLIP, :], table_quarters[q])
         offsets = held.tile([P, N // 16], U16, name="offsets")
         nc.sync.dma_start(offsets[:], offs)
 
-        b_in_row = held.tile([1, H], F32, name="b_in_row")
-        nc.sync.dma_start(b_in_row[:], b_in.rearrange("k one -> one k"))
         w_in_sb = held.tile([E, H], BF16, name="w_in_sb")
-        nc.scalar.dma_start(w_in_sb[:], w_in)
-        w_hid_sb = held.tile([H, H], BF16, name="w_hid_sb")
-        nc.scalar.dma_start(w_hid_sb[:], w_hid)
+        nc.sync.dma_start(w_in_sb[:], w_in)
         w_age_col = held.tile([H, 1], F32, name="w_age_col")
         nc.sync.dma_start(w_age_col[:], w_age)
+        b_in_col = held.tile([H, 1], F32, name="b_in_col")
+        nc.sync.dma_start(b_in_col[:], b_in)
+        w_hid_sb = held.tile([H, H], BF16, name="w_hid_sb")
+        nc.sync.dma_start(w_hid_sb[:], w_hid)
         b_hid_col = held.tile([H, 1], F32, name="b_hid_col")
-        nc.scalar.dma_start(b_hid_col[:], b_hid)
-        ages = [held.tile([P, N], F32, name=f"ages{t}") for t in range(D)]
-        for t in range(D):
-            queue = nc.sync if t % 2 == 0 else nc.scalar
-            queue.dma_start(ages[t][:], age[t, :].partition_broadcast(P))
+        nc.sync.dma_start(b_hid_col[:], b_hid)
 
         dummy = held.tile([P, 1], F32, name="dummy")
         nc.gpsimd.memset(dummy[:], 1.0)
         nc.scalar.sqrt(dummy[:], dummy[:])
         identity = held.tile([P, P], BF16, name="identity")
         masks.make_identity(nc, identity[:])
-        ones_row = held.tile([1, PIECE], F32, name="ones_row")
-        nc.gpsimd.memset(ones_row[:], 1.0)
-
-        proj = [proj_banks.tile([H, PIECE], F32, name=f"proj{g}") for g in range(PIECES)]
-        for g in range(PIECES):
-            nc.tensor.matmul(proj[g][:], b_in_row[:], ones_row[:], start=True, stop=False)
-
+        ages = [held.tile([P, N], F32, name=f"ages{t}") for t in range(D)]
+        for t in range(D):
+            nc.gpsimd.dma_start(ages[t][:], age[t, :].partition_broadcast(P))
         w_hid_minus = held.tile([H, H], BF16, name="w_hid_minus")
         nc.gpsimd.tensor_scalar_mul(w_hid_minus[:], w_hid_sb[:], -1.0)
         b_hid_low = held.tile([H, 1], F32, name="b_hid_low")
         nc.gpsimd.tensor_scalar_mul(b_hid_low[:], b_hid_col[:], SLOPE)
-        for t in range(D):
-            nc.gpsimd.tensor_scalar(ages[t][:], ages[t][:], FLT_MAX, 0.0, op0=MIN, op1=MAX)
 
         window = held.tile([E, S], BF16, name="window")
         with (
@@ -102,15 +90,22 @@ def tile_temporalnmf_kernel(tc, table, w_in, w_age, b_in, age, w_hid, b_hid, off
                         flipped[b // FLIP][:, (b % FLIP) * P : (b % FLIP + 1) * P], embs_rows[:, b, :], identity[:]
                     )
             for q in (0, 2, 1, 3):
-                columns = slice(q * PIECE, (q + 1) * PIECE)
+                in_order = window[:, q * PIECE : (q + 1) * PIECE].rearrange("e (p i) -> e p i", i=FLIP)
+                by_block = flipped[q][:].rearrange("e (i p) -> e p i", i=FLIP)
                 if q * FLIP < HALF:
-                    nc.vector.tensor_copy(window[:, columns], flipped[q][:])
+                    nc.vector.tensor_copy(in_order, by_block)
                 else:
-                    nc.scalar.copy(window[:, columns], flipped[q][:])
+                    nc.scalar.copy(in_order, by_block)
 
+        proj = [proj_banks.tile([H, PIECE], F32, name=f"proj{g}") for g in range(PIECES)]
         for g in range(PIECES):
             piece = offsets[:, g * (PIECE // 16) : (g + 1) * (PIECE // 16)]
-            nc.tensor.matmul(proj[g][:], w_in_sb[:], window[:].indirect(piece), start=False, stop=True)
+            nc.tensor.matmul(proj[g][:], w_in_sb[:], window[:].indirect(piece), start=True, stop=True)
+
+        def weigh_ages(t):
+            nc.vector.tensor_scalar(ages[t][:], ages[t][:], 0.0, w_age_col[:, 0:1], op0=MAX, op1=MULT)
+
+        weigh_ages(0)
 
         with (
             tc.tile_pool(name="work", bufs=4) as work,
@@ -123,20 +118,25 @@ def tile_temporalnmf_kernel(tc, table, w_in, w_age, b_in, age, w_hid, b_hid, off
                 z = work.tile([H, PIECE], F32, name="z")
                 nc.vector.scalar_tensor_tensor(
                     out=z[:],
-                    in0=ages[t][:, g * PIECE : (g + 1) * PIECE],
-                    scalar=w_age_col[:, 0:1],
-                    in1=proj[g][:],
-                    op0=MULT,
+                    in0=proj[g][:],
+                    scalar=b_in_col[:, 0:1],
+                    in1=ages[t][:, g * PIECE : (g + 1) * PIECE],
+                    op0=ADD,
                     op1=ADD,
                 )
                 h_plus = work.tile([H, PIECE], BF16, name="h_plus")
-                nc.gpsimd.tensor_scalar(h_plus[:], z[:], FLT_MAX, 0.0, op0=MIN, op1=MAX)
+                if g == 0:
+                    nc.vector.tensor_scalar_max(h_plus[:], z[:], 0.0)
+                else:
+                    nc.scalar.activation(h_plus[:], z[:], ACT.Relu)
                 h_minus = work.tile([H, PIECE], BF16, name="h_minus")
                 nc.scalar.activation(h_minus[:], z[:], ACT.Relu, scale=-SLOPE)
                 y = y_banks.tile([H, PIECE], F32, name="y")
                 nc.tensor.matmul(y[:], w_hid_sb[:], h_plus[:], start=True, stop=False)
                 nc.tensor.matmul(y[:], w_hid_minus[:], h_minus[:], start=False, stop=True)
                 products.append(y)
+                if g == PIECES - 1 and t + 1 < D:
+                    weigh_ages(t + 1)
 
             def second_layer(c):
                 y = products[c]

@@ -12,10 +12,11 @@ PIECE = 512
 PIECES = N // PIECE
 FLIP = PIECE // P
 LAG = 3
+FLT_MAX = 3.4028234663852886e38
 
 BF16, F32, U16 = mybir.dt.bfloat16, mybir.dt.float32, mybir.dt.uint16
 ADD, MULT = mybir.AluOpType.add, mybir.AluOpType.mult
-MAX = mybir.AluOpType.max
+MAX, MIN = mybir.AluOpType.max, mybir.AluOpType.min
 ACT = mybir.ActivationFunctionType
 
 
@@ -33,25 +34,37 @@ def tile_temporalnmf_kernel(tc, table, w_in, w_age, b_in, age, w_hid, b_hid, off
         offsets = held.tile([P, N // 16], U16, name="offsets")
         nc.sync.dma_start(offsets[:], offs)
 
+        b_in_row = held.tile([1, H], F32, name="b_in_row")
+        nc.sync.dma_start(b_in_row[:], b_in.rearrange("k one -> one k"))
         w_in_sb = held.tile([E, H], BF16, name="w_in_sb")
         nc.sync.dma_start(w_in_sb[:], w_in)
         w_age_col = held.tile([H, 1], F32, name="w_age_col")
         nc.sync.dma_start(w_age_col[:], w_age)
-        b_in_col = held.tile([H, 1], F32, name="b_in_col")
-        nc.sync.dma_start(b_in_col[:], b_in)
         w_hid_sb = held.tile([H, H], BF16, name="w_hid_sb")
         nc.sync.dma_start(w_hid_sb[:], w_hid)
         b_hid_col = held.tile([H, 1], F32, name="b_hid_col")
         nc.sync.dma_start(b_hid_col[:], b_hid)
+        ages = [held.tile([P, N], F32, name=f"ages{t}") for t in range(D)]
+        for t in range(D):
+            nc.sync.dma_start(ages[t][:], age[t, :].partition_broadcast(P))
 
         dummy = held.tile([P, 1], F32, name="dummy")
         nc.gpsimd.memset(dummy[:], 1.0)
         nc.scalar.sqrt(dummy[:], dummy[:])
         identity = held.tile([P, P], BF16, name="identity")
         masks.make_identity(nc, identity[:])
-        ages = [held.tile([P, N], F32, name=f"ages{t}") for t in range(D)]
-        for t in range(D):
-            nc.gpsimd.dma_start(ages[t][:], age[t, :].partition_broadcast(P))
+        ones_row = held.tile([1, PIECE], F32, name="ones_row")
+        nc.gpsimd.memset(ones_row[:], 1.0)
+
+        proj = [proj_banks.tile([H, PIECE], F32, name=f"proj{g}") for g in range(PIECES)]
+        for g in range(PIECES):
+            nc.tensor.matmul(proj[g][:], b_in_row[:], ones_row[:], start=True, stop=False)
+
+        def clamp_ages(t):
+            nc.gpsimd.tensor_scalar(ages[t][:], ages[t][:], FLT_MAX, 0.0, op0=MIN, op1=MAX)
+
+        clamp_ages(0)
+        clamp_ages(1)
         w_hid_minus = held.tile([H, H], BF16, name="w_hid_minus")
         nc.gpsimd.tensor_scalar_mul(w_hid_minus[:], w_hid_sb[:], -1.0)
         b_hid_low = held.tile([H, 1], F32, name="b_hid_low")
@@ -97,15 +110,9 @@ def tile_temporalnmf_kernel(tc, table, w_in, w_age, b_in, age, w_hid, b_hid, off
                 else:
                     nc.scalar.copy(in_order, by_block)
 
-        proj = [proj_banks.tile([H, PIECE], F32, name=f"proj{g}") for g in range(PIECES)]
         for g in range(PIECES):
             piece = offsets[:, g * (PIECE // 16) : (g + 1) * (PIECE // 16)]
-            nc.tensor.matmul(proj[g][:], w_in_sb[:], window[:].indirect(piece), start=True, stop=True)
-
-        def weigh_ages(t):
-            nc.vector.tensor_scalar(ages[t][:], ages[t][:], 0.0, w_age_col[:, 0:1], op0=MAX, op1=MULT)
-
-        weigh_ages(0)
+            nc.tensor.matmul(proj[g][:], w_in_sb[:], window[:].indirect(piece), start=False, stop=True)
 
         with (
             tc.tile_pool(name="work", bufs=4) as work,
@@ -118,25 +125,22 @@ def tile_temporalnmf_kernel(tc, table, w_in, w_age, b_in, age, w_hid, b_hid, off
                 z = work.tile([H, PIECE], F32, name="z")
                 nc.vector.scalar_tensor_tensor(
                     out=z[:],
-                    in0=proj[g][:],
-                    scalar=b_in_col[:, 0:1],
-                    in1=ages[t][:, g * PIECE : (g + 1) * PIECE],
-                    op0=ADD,
+                    in0=ages[t][:, g * PIECE : (g + 1) * PIECE],
+                    scalar=w_age_col[:, 0:1],
+                    in1=proj[g][:],
+                    op0=MULT,
                     op1=ADD,
                 )
                 h_plus = work.tile([H, PIECE], BF16, name="h_plus")
-                if g == 0:
-                    nc.vector.tensor_scalar_max(h_plus[:], z[:], 0.0)
-                else:
-                    nc.scalar.activation(h_plus[:], z[:], ACT.Relu)
+                nc.gpsimd.tensor_scalar(h_plus[:], z[:], FLT_MAX, 0.0, op0=MIN, op1=MAX)
                 h_minus = work.tile([H, PIECE], BF16, name="h_minus")
                 nc.scalar.activation(h_minus[:], z[:], ACT.Relu, scale=-SLOPE)
                 y = y_banks.tile([H, PIECE], F32, name="y")
                 nc.tensor.matmul(y[:], w_hid_sb[:], h_plus[:], start=True, stop=False)
                 nc.tensor.matmul(y[:], w_hid_minus[:], h_minus[:], start=False, stop=True)
                 products.append(y)
-                if g == PIECES - 1 and t + 1 < D:
-                    weigh_ages(t + 1)
+                if g == PIECES - 1 and t + 2 < D:
+                    clamp_ages(t + 2)
 
             def second_layer(c):
                 y = products[c]

@@ -34,12 +34,12 @@ def tile_temporalnmf_kernel(tc, table, w_in, w_age, b_in, age, w_hid, b_hid, off
         offsets = held.tile([P, N // 16], U16, name="offsets")
         nc.sync.dma_start(offsets[:], offs)
 
-        b_in_row = held.tile([1, H], F32, name="b_in_row")
-        nc.sync.dma_start(b_in_row[:], b_in.rearrange("k one -> one k"))
         w_in_sb = held.tile([E, H], BF16, name="w_in_sb")
         nc.sync.dma_start(w_in_sb[:], w_in)
         w_age_col = held.tile([H, 1], F32, name="w_age_col")
         nc.sync.dma_start(w_age_col[:], w_age)
+        b_in_col = held.tile([H, 1], F32, name="b_in_col")
+        nc.sync.dma_start(b_in_col[:], b_in)
         w_hid_sb = held.tile([H, H], BF16, name="w_hid_sb")
         nc.sync.dma_start(w_hid_sb[:], w_hid)
         b_hid_col = held.tile([H, 1], F32, name="b_hid_col")
@@ -53,18 +53,6 @@ def tile_temporalnmf_kernel(tc, table, w_in, w_age, b_in, age, w_hid, b_hid, off
         nc.scalar.sqrt(dummy[:], dummy[:])
         identity = held.tile([P, P], BF16, name="identity")
         masks.make_identity(nc, identity[:])
-        ones_row = held.tile([1, PIECE], F32, name="ones_row")
-        nc.gpsimd.memset(ones_row[:], 1.0)
-
-        proj = [proj_banks.tile([H, PIECE], F32, name=f"proj{g}") for g in range(PIECES)]
-        for g in range(PIECES):
-            nc.tensor.matmul(proj[g][:], b_in_row[:], ones_row[:], start=True, stop=False)
-
-        def clamp_ages(t):
-            nc.gpsimd.tensor_scalar(ages[t][:], ages[t][:], FLT_MAX, 0.0, op0=MIN, op1=MAX)
-
-        clamp_ages(0)
-        clamp_ages(1)
         w_hid_minus = held.tile([H, H], BF16, name="w_hid_minus")
         nc.gpsimd.tensor_scalar_mul(w_hid_minus[:], w_hid_sb[:], -1.0)
         b_hid_low = held.tile([H, 1], F32, name="b_hid_low")
@@ -110,9 +98,13 @@ def tile_temporalnmf_kernel(tc, table, w_in, w_age, b_in, age, w_hid, b_hid, off
                 else:
                     nc.scalar.copy(in_order, by_block)
 
+        proj = [proj_banks.tile([H, PIECE], F32, name=f"proj{g}") for g in range(PIECES)]
         for g in range(PIECES):
             piece = offsets[:, g * (PIECE // 16) : (g + 1) * (PIECE // 16)]
-            nc.tensor.matmul(proj[g][:], w_in_sb[:], window[:].indirect(piece), start=False, stop=True)
+            nc.tensor.matmul(proj[g][:], w_in_sb[:], window[:].indirect(piece), start=True, stop=True)
+
+        for t in range(D):
+            nc.vector.tensor_scalar(ages[t][:], ages[t][:], 0.0, w_age_col[:, 0:1], op0=MAX, op1=MULT)
 
         with (
             tc.tile_pool(name="work", bufs=4) as work,
@@ -125,10 +117,10 @@ def tile_temporalnmf_kernel(tc, table, w_in, w_age, b_in, age, w_hid, b_hid, off
                 z = work.tile([H, PIECE], F32, name="z")
                 nc.vector.scalar_tensor_tensor(
                     out=z[:],
-                    in0=ages[t][:, g * PIECE : (g + 1) * PIECE],
-                    scalar=w_age_col[:, 0:1],
-                    in1=proj[g][:],
-                    op0=MULT,
+                    in0=proj[g][:],
+                    scalar=b_in_col[:, 0:1],
+                    in1=ages[t][:, g * PIECE : (g + 1) * PIECE],
+                    op0=ADD,
                     op1=ADD,
                 )
                 h_plus = work.tile([H, PIECE], BF16, name="h_plus")
@@ -139,8 +131,6 @@ def tile_temporalnmf_kernel(tc, table, w_in, w_age, b_in, age, w_hid, b_hid, off
                 nc.tensor.matmul(y[:], w_hid_sb[:], h_plus[:], start=True, stop=False)
                 nc.tensor.matmul(y[:], w_hid_minus[:], h_minus[:], start=False, stop=True)
                 products.append(y)
-                if g == PIECES - 1 and t + 2 < D:
-                    clamp_ages(t + 2)
 
             def second_layer(c):
                 y = products[c]

@@ -11,6 +11,8 @@ HALF = BLOCKS // 2
 PIECE = 512
 PIECES = N // PIECE
 FLIP = PIECE // P
+QUARTERS = BLOCKS // FLIP
+SHARE = FLIP // 2
 LAG = 3
 FLT_MAX = 3.4028234663852886e38
 
@@ -28,8 +30,10 @@ def tile_temporalnmf_kernel(tc, table, w_in, w_age, b_in, age, w_hid, b_hid, off
     ):
         table_quarters = table.rearrange("(q p i) e -> q p i e", p=P, i=FLIP)
         rows = held.tile([P, BLOCKS, E], BF16, name="rows")
-        for q in (0, 2, 1, 3):
-            queue = nc.sync if q * FLIP < HALF else nc.scalar
+        b_in_rows = held.tile([P, H], F32, name="b_in_rows")
+        nc.sync.dma_start(b_in_rows[:], b_in.rearrange("k one -> (k one)").partition_broadcast(P))
+        for q in range(QUARTERS):
+            queue = nc.sync if q % 2 == 0 else nc.scalar
             queue.dma_start(rows[:, q * FLIP : (q + 1) * FLIP, :], table_quarters[q])
         offsets = held.tile([P, N // 16], U16, name="offsets")
         nc.sync.dma_start(offsets[:], offs)
@@ -38,8 +42,6 @@ def tile_temporalnmf_kernel(tc, table, w_in, w_age, b_in, age, w_hid, b_hid, off
         nc.sync.dma_start(w_in_sb[:], w_in)
         w_age_col = held.tile([H, 1], F32, name="w_age_col")
         nc.sync.dma_start(w_age_col[:], w_age)
-        b_in_col = held.tile([H, 1], F32, name="b_in_col")
-        nc.sync.dma_start(b_in_col[:], b_in)
         w_hid_sb = held.tile([H, H], BF16, name="w_hid_sb")
         nc.sync.dma_start(w_hid_sb[:], w_hid)
         b_hid_col = held.tile([H, 1], F32, name="b_hid_col")
@@ -53,10 +55,19 @@ def tile_temporalnmf_kernel(tc, table, w_in, w_age, b_in, age, w_hid, b_hid, off
         nc.scalar.sqrt(dummy[:], dummy[:])
         identity = held.tile([P, P], BF16, name="identity")
         masks.make_identity(nc, identity[:])
+        first_only = held.tile([P, PIECE], F32, name="first_only")
+        nc.vector.memset(first_only[:], 0.0)
+        nc.vector.memset(first_only[0:1, :], 1.0)
+        proj = [proj_banks.tile([H, PIECE], F32, name=f"proj{g}") for g in range(PIECES)]
+        for g in range(PIECES):
+            nc.tensor.matmul(proj[g][:], b_in_rows[:], first_only[:], start=True, stop=False)
+
         w_hid_minus = held.tile([H, H], BF16, name="w_hid_minus")
         nc.gpsimd.tensor_scalar_mul(w_hid_minus[:], w_hid_sb[:], -1.0)
         b_hid_low = held.tile([H, 1], F32, name="b_hid_low")
         nc.gpsimd.tensor_scalar_mul(b_hid_low[:], b_hid_col[:], SLOPE)
+        for t in range(D):
+            nc.gpsimd.tensor_scalar(ages[t][:], ages[t][:], FLT_MAX, 0.0, op0=MIN, op1=MAX)
 
         window = held.tile([E, S], BF16, name="window")
         with (
@@ -65,46 +76,59 @@ def tile_temporalnmf_kernel(tc, table, w_in, w_age, b_in, age, w_hid, b_hid, off
         ):
             squares = shrinking.tile([P, BLOCKS, E], F32, name="squares")
             sumsq = shrinking.tile([P, BLOCKS], F32, name="sumsq")
-            for quarter in range(2):
-                blocks = slice(quarter * FLIP, (quarter + 1) * FLIP)
-                nc.vector.tensor_tensor(squares[:, blocks, :], rows[:, blocks, :], rows[:, blocks, :], MULT)
-                nc.vector.reduce_sum(sumsq[:, blocks], squares[:, blocks, :], axis=mybir.AxisListType.X)
-            for b in range(HALF, BLOCKS):
-                nc.scalar.activation(squares[:, b, :], rows[:, b, :], ACT.Square, accum_out=sumsq[:, b : b + 1])
-
             norm = shrinking.tile([P, BLOCKS], F32, name="norm")
-            nc.scalar.sqrt(norm[:], sumsq[:])
             divisor = shrinking.tile([P, BLOCKS], F32, name="divisor")
-            nc.vector.tensor_scalar(divisor[:], norm[:], EPS, 1.0, op0=ADD, op1=MAX)
             factor = shrinking.tile([P, BLOCKS], F32, name="factor")
-            nc.vector.reciprocal(factor[:], divisor[:])
-
             embs_rows = shrinking.tile([P, BLOCKS, E], BF16, name="embs_rows")
-            flipped = [flip_banks.tile([E, PIECE], BF16, name=f"flipped{q}") for q in range(BLOCKS // FLIP)]
-            for i in range(HALF):
-                for b in (i, HALF + i):
-                    if b < HALF:
-                        nc.vector.tensor_scalar(embs_rows[:, b, :], rows[:, b, :], factor[:, b : b + 1], None, op0=MULT)
-                    else:
-                        nc.scalar.activation(embs_rows[:, b, :], rows[:, b, :], ACT.Copy, scale=factor[:, b : b + 1])
-                    nc.tensor.transpose(
-                        flipped[b // FLIP][:, (b % FLIP) * P : (b % FLIP + 1) * P], embs_rows[:, b, :], identity[:]
+            flipped = [flip_banks.tile([E, PIECE], F32, name=f"flipped{q}") for q in range(QUARTERS)]
+
+            def of_quarter(per_block, q):
+                return per_block[:].rearrange("p (half q c) -> p half q c", half=2, q=QUARTERS)[:, :, q, :]
+
+            for q in range(QUARTERS):
+                first = q * FLIP
+                v_blocks = slice(first, first + SHARE)
+                v_columns = slice(q * SHARE, (q + 1) * SHARE)
+                nc.vector.tensor_tensor(squares[:, v_blocks, :], rows[:, v_blocks, :], rows[:, v_blocks, :], MULT)
+                nc.vector.reduce_sum(sumsq[:, v_columns], squares[:, v_blocks, :], axis=mybir.AxisListType.X)
+                for c in range(SHARE):
+                    b = first + SHARE + c
+                    column = HALF + q * SHARE + c
+                    nc.scalar.activation(
+                        squares[:, b, :], rows[:, b, :], ACT.Square, accum_out=sumsq[:, column : column + 1]
                     )
-            for q in (0, 2, 1, 3):
+
+                nc.scalar.sqrt(of_quarter(norm, q), of_quarter(sumsq, q))
+                nc.vector.tensor_scalar(of_quarter(divisor, q), of_quarter(norm, q), EPS, 1.0, op0=ADD, op1=MAX)
+                nc.vector.reciprocal(of_quarter(factor, q), of_quarter(divisor, q))
+
+                for c in range(SHARE):
+                    for i in (c, SHARE + c):
+                        b = first + i
+                        if i < SHARE:
+                            column = q * SHARE + c
+                            nc.vector.tensor_scalar(
+                                embs_rows[:, b, :], rows[:, b, :], factor[:, column : column + 1], None, op0=MULT
+                            )
+                        else:
+                            column = HALF + q * SHARE + c
+                            nc.scalar.activation(
+                                embs_rows[:, b, :], rows[:, b, :], ACT.Copy, scale=factor[:, column : column + 1]
+                            )
+                        nc.tensor.matmul(
+                            flipped[q][:, i * P : (i + 1) * P], embs_rows[:, b, :], identity[:], start=True, stop=True
+                        )
+
                 in_order = window[:, q * PIECE : (q + 1) * PIECE].rearrange("e (p i) -> e p i", i=FLIP)
                 by_block = flipped[q][:].rearrange("e (i p) -> e p i", i=FLIP)
-                if q * FLIP < HALF:
+                if q % 2 == 0:
                     nc.vector.tensor_copy(in_order, by_block)
                 else:
                     nc.scalar.copy(in_order, by_block)
 
-        proj = [proj_banks.tile([H, PIECE], F32, name=f"proj{g}") for g in range(PIECES)]
         for g in range(PIECES):
             piece = offsets[:, g * (PIECE // 16) : (g + 1) * (PIECE // 16)]
-            nc.tensor.matmul(proj[g][:], w_in_sb[:], window[:].indirect(piece), start=True, stop=True)
-
-        for t in range(D):
-            nc.vector.tensor_scalar(ages[t][:], ages[t][:], 0.0, w_age_col[:, 0:1], op0=MAX, op1=MULT)
+            nc.tensor.matmul(proj[g][:], w_in_sb[:], window[:].indirect(piece), start=False, stop=True)
 
         with (
             tc.tile_pool(name="work", bufs=4) as work,
@@ -117,10 +141,10 @@ def tile_temporalnmf_kernel(tc, table, w_in, w_age, b_in, age, w_hid, b_hid, off
                 z = work.tile([H, PIECE], F32, name="z")
                 nc.vector.scalar_tensor_tensor(
                     out=z[:],
-                    in0=proj[g][:],
-                    scalar=b_in_col[:, 0:1],
-                    in1=ages[t][:, g * PIECE : (g + 1) * PIECE],
-                    op0=ADD,
+                    in0=ages[t][:, g * PIECE : (g + 1) * PIECE],
+                    scalar=w_age_col[:, 0:1],
+                    in1=proj[g][:],
+                    op0=MULT,
                     op1=ADD,
                 )
                 h_plus = work.tile([H, PIECE], BF16, name="h_plus")

@@ -11,8 +11,6 @@ HALF = BLOCKS // 2
 PIECE = 512
 PIECES = N // PIECE
 FLIP = PIECE // P
-QUARTERS = BLOCKS // FLIP
-SHARE = FLIP // 2
 LAG = 3
 FLT_MAX = 3.4028234663852886e38
 
@@ -30,44 +28,36 @@ def tile_temporalnmf_kernel(tc, table, w_in, w_age, b_in, age, w_hid, b_hid, off
     ):
         table_quarters = table.rearrange("(q p i) e -> q p i e", p=P, i=FLIP)
         rows = held.tile([P, BLOCKS, E], BF16, name="rows")
-        b_in_rows = held.tile([P, H], F32, name="b_in_rows")
-        nc.sync.dma_start(b_in_rows[:], b_in.rearrange("k one -> (k one)").partition_broadcast(P))
-        for q in range(QUARTERS):
-            queue = nc.sync if q % 2 == 0 else nc.scalar
+        for q in (0, 2, 1, 3):
+            queue = nc.sync if q * FLIP < HALF else nc.scalar
             queue.dma_start(rows[:, q * FLIP : (q + 1) * FLIP, :], table_quarters[q])
-        offsets = held.tile([P, N // 16], U16, name="offsets")
-        nc.sync.dma_start(offsets[:], offs)
-
-        w_in_sb = held.tile([E, H], BF16, name="w_in_sb")
-        nc.sync.dma_start(w_in_sb[:], w_in)
         w_age_col = held.tile([H, 1], F32, name="w_age_col")
         nc.sync.dma_start(w_age_col[:], w_age)
+        ages = [held.tile([P, N], F32, name=f"ages{t}") for t in range(D)]
+        for t in range(D // 2):
+            nc.sync.dma_start(ages[t][:], age[t, :].partition_broadcast(P))
+        offsets = held.tile([P, N // 16], U16, name="offsets")
+        nc.sync.dma_start(offsets[:], offs)
+        w_in_sb = held.tile([E, H], BF16, name="w_in_sb")
+        nc.sync.dma_start(w_in_sb[:], w_in)
+        for t in range(D // 2, D):
+            nc.sync.dma_start(ages[t][:], age[t, :].partition_broadcast(P))
+        b_in_col = held.tile([H, 1], F32, name="b_in_col")
+        nc.sync.dma_start(b_in_col[:], b_in)
         w_hid_sb = held.tile([H, H], BF16, name="w_hid_sb")
         nc.sync.dma_start(w_hid_sb[:], w_hid)
         b_hid_col = held.tile([H, 1], F32, name="b_hid_col")
         nc.sync.dma_start(b_hid_col[:], b_hid)
-        ages = [held.tile([P, N], F32, name=f"ages{t}") for t in range(D)]
-        for t in range(D):
-            nc.sync.dma_start(ages[t][:], age[t, :].partition_broadcast(P))
 
         dummy = held.tile([P, 1], F32, name="dummy")
         nc.gpsimd.memset(dummy[:], 1.0)
         nc.scalar.sqrt(dummy[:], dummy[:])
         identity = held.tile([P, P], BF16, name="identity")
         masks.make_identity(nc, identity[:])
-        first_only = held.tile([P, PIECE], F32, name="first_only")
-        nc.vector.memset(first_only[:], 0.0)
-        nc.vector.memset(first_only[0:1, :], 1.0)
-        proj = [proj_banks.tile([H, PIECE], F32, name=f"proj{g}") for g in range(PIECES)]
-        for g in range(PIECES):
-            nc.tensor.matmul(proj[g][:], b_in_rows[:], first_only[:], start=True, stop=False)
-
         w_hid_minus = held.tile([H, H], BF16, name="w_hid_minus")
         nc.gpsimd.tensor_scalar_mul(w_hid_minus[:], w_hid_sb[:], -1.0)
         b_hid_low = held.tile([H, 1], F32, name="b_hid_low")
         nc.gpsimd.tensor_scalar_mul(b_hid_low[:], b_hid_col[:], SLOPE)
-        for t in range(D):
-            nc.gpsimd.tensor_scalar(ages[t][:], ages[t][:], FLT_MAX, 0.0, op0=MIN, op1=MAX)
 
         window = held.tile([E, S], BF16, name="window")
         with (
@@ -76,59 +66,46 @@ def tile_temporalnmf_kernel(tc, table, w_in, w_age, b_in, age, w_hid, b_hid, off
         ):
             squares = shrinking.tile([P, BLOCKS, E], F32, name="squares")
             sumsq = shrinking.tile([P, BLOCKS], F32, name="sumsq")
+            for quarter in range(2):
+                blocks = slice(quarter * FLIP, (quarter + 1) * FLIP)
+                nc.vector.tensor_tensor(squares[:, blocks, :], rows[:, blocks, :], rows[:, blocks, :], MULT)
+                nc.vector.reduce_sum(sumsq[:, blocks], squares[:, blocks, :], axis=mybir.AxisListType.X)
+            for b in range(HALF, BLOCKS):
+                nc.scalar.activation(squares[:, b, :], rows[:, b, :], ACT.Square, accum_out=sumsq[:, b : b + 1])
+
             norm = shrinking.tile([P, BLOCKS], F32, name="norm")
+            nc.scalar.sqrt(norm[:], sumsq[:])
             divisor = shrinking.tile([P, BLOCKS], F32, name="divisor")
+            nc.vector.tensor_scalar(divisor[:], norm[:], EPS, 1.0, op0=ADD, op1=MAX)
             factor = shrinking.tile([P, BLOCKS], F32, name="factor")
+            nc.vector.reciprocal(factor[:], divisor[:])
+
             embs_rows = shrinking.tile([P, BLOCKS, E], BF16, name="embs_rows")
-            flipped = [flip_banks.tile([E, PIECE], F32, name=f"flipped{q}") for q in range(QUARTERS)]
-
-            def of_quarter(per_block, q):
-                return per_block[:].rearrange("p (half q c) -> p half q c", half=2, q=QUARTERS)[:, :, q, :]
-
-            for q in range(QUARTERS):
-                first = q * FLIP
-                v_blocks = slice(first, first + SHARE)
-                v_columns = slice(q * SHARE, (q + 1) * SHARE)
-                nc.vector.tensor_tensor(squares[:, v_blocks, :], rows[:, v_blocks, :], rows[:, v_blocks, :], MULT)
-                nc.vector.reduce_sum(sumsq[:, v_columns], squares[:, v_blocks, :], axis=mybir.AxisListType.X)
-                for c in range(SHARE):
-                    b = first + SHARE + c
-                    column = HALF + q * SHARE + c
-                    nc.scalar.activation(
-                        squares[:, b, :], rows[:, b, :], ACT.Square, accum_out=sumsq[:, column : column + 1]
+            flipped = [flip_banks.tile([E, PIECE], BF16, name=f"flipped{q}") for q in range(BLOCKS // FLIP)]
+            for i in range(HALF):
+                for b in (i, HALF + i):
+                    if b < HALF:
+                        nc.vector.tensor_scalar(embs_rows[:, b, :], rows[:, b, :], factor[:, b : b + 1], None, op0=MULT)
+                    else:
+                        nc.scalar.activation(embs_rows[:, b, :], rows[:, b, :], ACT.Copy, scale=factor[:, b : b + 1])
+                    nc.tensor.transpose(
+                        flipped[b // FLIP][:, (b % FLIP) * P : (b % FLIP + 1) * P], embs_rows[:, b, :], identity[:]
                     )
-
-                nc.scalar.sqrt(of_quarter(norm, q), of_quarter(sumsq, q))
-                nc.vector.tensor_scalar(of_quarter(divisor, q), of_quarter(norm, q), EPS, 1.0, op0=ADD, op1=MAX)
-                nc.vector.reciprocal(of_quarter(factor, q), of_quarter(divisor, q))
-
-                for c in range(SHARE):
-                    for i in (c, SHARE + c):
-                        b = first + i
-                        if i < SHARE:
-                            column = q * SHARE + c
-                            nc.vector.tensor_scalar(
-                                embs_rows[:, b, :], rows[:, b, :], factor[:, column : column + 1], None, op0=MULT
-                            )
-                        else:
-                            column = HALF + q * SHARE + c
-                            nc.scalar.activation(
-                                embs_rows[:, b, :], rows[:, b, :], ACT.Copy, scale=factor[:, column : column + 1]
-                            )
-                        nc.tensor.matmul(
-                            flipped[q][:, i * P : (i + 1) * P], embs_rows[:, b, :], identity[:], start=True, stop=True
-                        )
-
+            for q in (0, 2, 1, 3):
                 in_order = window[:, q * PIECE : (q + 1) * PIECE].rearrange("e (p i) -> e p i", i=FLIP)
                 by_block = flipped[q][:].rearrange("e (i p) -> e p i", i=FLIP)
-                if q % 2 == 0:
+                if q * FLIP < HALF:
                     nc.vector.tensor_copy(in_order, by_block)
                 else:
                     nc.scalar.copy(in_order, by_block)
 
+        proj = [proj_banks.tile([H, PIECE], F32, name=f"proj{g}") for g in range(PIECES)]
         for g in range(PIECES):
             piece = offsets[:, g * (PIECE // 16) : (g + 1) * (PIECE // 16)]
-            nc.tensor.matmul(proj[g][:], w_in_sb[:], window[:].indirect(piece), start=False, stop=True)
+            nc.tensor.matmul(proj[g][:], w_in_sb[:], window[:].indirect(piece), start=True, stop=True)
+
+        for t in range(D):
+            nc.vector.tensor_scalar(ages[t][:], ages[t][:], 0.0, w_age_col[:, 0:1], op0=MAX, op1=MULT)
 
         with (
             tc.tile_pool(name="work", bufs=4) as work,
@@ -141,10 +118,10 @@ def tile_temporalnmf_kernel(tc, table, w_in, w_age, b_in, age, w_hid, b_hid, off
                 z = work.tile([H, PIECE], F32, name="z")
                 nc.vector.scalar_tensor_tensor(
                     out=z[:],
-                    in0=ages[t][:, g * PIECE : (g + 1) * PIECE],
-                    scalar=w_age_col[:, 0:1],
-                    in1=proj[g][:],
-                    op0=MULT,
+                    in0=proj[g][:],
+                    scalar=b_in_col[:, 0:1],
+                    in1=ages[t][:, g * PIECE : (g + 1) * PIECE],
+                    op0=ADD,
                     op1=ADD,
                 )
                 h_plus = work.tile([H, PIECE], BF16, name="h_plus")

@@ -66,10 +66,16 @@ def tile_temporalnmf_kernel(tc, table, w_in, w_age, b_in, age, w_hid, b_hid, off
         ):
             squares = shrinking.tile([P, BLOCKS, E], F32, name="squares")
             sumsq = shrinking.tile([P, BLOCKS], F32, name="sumsq")
-            for quarter in range(2):
-                blocks = slice(quarter * FLIP, (quarter + 1) * FLIP)
-                nc.vector.tensor_tensor(squares[:, blocks, :], rows[:, blocks, :], rows[:, blocks, :], MULT)
-                nc.vector.reduce_sum(sumsq[:, blocks], squares[:, blocks, :], axis=mybir.AxisListType.X)
+            for b in range(HALF):
+                nc.vector.scalar_tensor_tensor(
+                    out=squares[:, b, :],
+                    in0=rows[:, b, :],
+                    scalar=1.0,
+                    in1=rows[:, b, :],
+                    op0=MULT,
+                    op1=MULT,
+                    accum_out=sumsq[:, b : b + 1],
+                )
             for b in range(HALF, BLOCKS):
                 nc.scalar.activation(squares[:, b, :], rows[:, b, :], ACT.Square, accum_out=sumsq[:, b : b + 1])
 
@@ -109,6 +115,7 @@ def tile_temporalnmf_kernel(tc, table, w_in, w_age, b_in, age, w_hid, b_hid, off
 
         with (
             tc.tile_pool(name="work", bufs=4) as work,
+            tc.tile_pool(name="results", bufs=D * PIECES) as results,
             tc.psum_pool(name="y_banks", bufs=LAG + 2) as y_banks,
         ):
             chunks = [(t, g) for t in range(D) for g in range(PIECES)]
@@ -127,7 +134,10 @@ def tile_temporalnmf_kernel(tc, table, w_in, w_age, b_in, age, w_hid, b_hid, off
                 h_plus = work.tile([H, PIECE], BF16, name="h_plus")
                 nc.gpsimd.tensor_scalar(h_plus[:], z[:], FLT_MAX, 0.0, op0=MIN, op1=MAX)
                 h_minus = work.tile([H, PIECE], BF16, name="h_minus")
-                nc.scalar.activation(h_minus[:], z[:], ACT.Relu, scale=-SLOPE)
+                if len(products) % 4 == 3:
+                    nc.vector.tensor_scalar(h_minus[:], z[:], -SLOPE, 0.0, op0=MULT, op1=MAX)
+                else:
+                    nc.scalar.activation(h_minus[:], z[:], ACT.Relu, scale=-SLOPE)
                 y = y_banks.tile([H, PIECE], F32, name="y")
                 nc.tensor.matmul(y[:], w_hid_sb[:], h_plus[:], start=True, stop=False)
                 nc.tensor.matmul(y[:], w_hid_minus[:], h_minus[:], start=False, stop=True)
@@ -137,7 +147,7 @@ def tile_temporalnmf_kernel(tc, table, w_in, w_age, b_in, age, w_hid, b_hid, off
                 y = products[c]
                 low = work.tile([H, PIECE], F32, name="low")
                 nc.scalar.activation(low[:], y[:], ACT.Identity, bias=b_hid_low[:, 0:1], scale=SLOPE)
-                result = work.tile([H, PIECE], F32, name="result")
+                result = results.tile([H, PIECE], F32, name="result")
                 nc.vector.scalar_tensor_tensor(
                     out=result[:], in0=y[:], scalar=b_hid_col[:, 0:1], in1=low[:], op0=ADD, op1=MAX
                 )

@@ -33,6 +33,8 @@ def tile_temporalnmf_kernel(tc, table, w_in, w_age, b_in, age, w_hid, b_hid, off
             queue.dma_start(rows[:, q * FLIP : (q + 1) * FLIP, :], table_quarters[q])
         w_age_col = held.tile([H, 1], F32, name="w_age_col")
         nc.sync.dma_start(w_age_col[:], w_age)
+        b_in_col = held.tile([H, 1], F32, name="b_in_col")
+        nc.sync.dma_start(b_in_col[:], b_in)
         ages = [held.tile([P, N], F32, name=f"ages{t}") for t in range(D)]
         for t in range(D // 2):
             nc.sync.dma_start(ages[t][:], age[t, :].partition_broadcast(P))
@@ -42,8 +44,6 @@ def tile_temporalnmf_kernel(tc, table, w_in, w_age, b_in, age, w_hid, b_hid, off
         nc.sync.dma_start(w_in_sb[:], w_in)
         for t in range(D // 2, D):
             nc.sync.dma_start(ages[t][:], age[t, :].partition_broadcast(P))
-        b_in_col = held.tile([H, 1], F32, name="b_in_col")
-        nc.sync.dma_start(b_in_col[:], b_in)
         w_hid_sb = held.tile([H, H], BF16, name="w_hid_sb")
         nc.sync.dma_start(w_hid_sb[:], w_hid)
         b_hid_col = held.tile([H, 1], F32, name="b_hid_col")
@@ -110,8 +110,10 @@ def tile_temporalnmf_kernel(tc, table, w_in, w_age, b_in, age, w_hid, b_hid, off
             piece = offsets[:, g * (PIECE // 16) : (g + 1) * (PIECE // 16)]
             nc.tensor.matmul(proj[g][:], w_in_sb[:], window[:].indirect(piece), start=True, stop=True)
 
-        for t in range(D):
+        def weigh(t):
             nc.vector.tensor_scalar(ages[t][:], ages[t][:], 0.0, w_age_col[:, 0:1], op0=MAX, op1=MULT)
+
+        weigh(0)
 
         with (
             tc.tile_pool(name="work", bufs=4) as work,
@@ -131,6 +133,8 @@ def tile_temporalnmf_kernel(tc, table, w_in, w_age, b_in, age, w_hid, b_hid, off
                     op0=ADD,
                     op1=ADD,
                 )
+                if g == 0 and t + 1 < D:
+                    weigh(t + 1)
                 h_plus = work.tile([H, PIECE], BF16, name="h_plus")
                 nc.gpsimd.tensor_scalar(h_plus[:], z[:], FLT_MAX, 0.0, op0=MIN, op1=MAX)
                 h_minus = work.tile([H, PIECE], BF16, name="h_minus")

@@ -64,7 +64,7 @@ def tile_temporalnmf_kernel(tc, table, w_in, w_age, b_in, age, w_hid, b_hid, off
             tc.tile_pool(name="shrinking", bufs=1) as shrinking,
             tc.psum_pool(name="flip_banks", bufs=1) as flip_banks,
         ):
-            squares = shrinking.tile([P, BLOCKS, E], F32, name="squares")
+            squares = shrinking.tile([P, BLOCKS, E], BF16, name="squares")
             sumsq = shrinking.tile([P, BLOCKS], F32, name="sumsq")
             for b in range(HALF):
                 nc.vector.scalar_tensor_tensor(

@@ -6,16 +6,21 @@ SLOPE, EPS = 0.3, 1e-7
 FLOPS = 2 * E * H * N + 2 * H * H * D * N
 
 P = 128
-BLOCKS = S // P
-HALF = BLOCKS // 2
+QUADRANT = 32
 PIECE = 512
 PIECES = N // PIECE
+CHUNKS = D * PIECES
 FLIP = PIECE // P
-LAG = 3
+BLOCKS = S // P
+QUARTERS = BLOCKS // FLIP
+STRIP = D * N // QUADRANT
+STRIPS = PIECE // STRIP
+LAG = 6
+AHEAD = 4
 FLT_MAX = 3.4028234663852886e38
 
 BF16, F32, U16 = mybir.dt.bfloat16, mybir.dt.float32, mybir.dt.uint16
-ADD, MULT = mybir.AluOpType.add, mybir.AluOpType.mult
+ADD, MULT, SUB = mybir.AluOpType.add, mybir.AluOpType.mult, mybir.AluOpType.subtract
 MAX, MIN = mybir.AluOpType.max, mybir.AluOpType.min
 ACT = mybir.ActivationFunctionType
 
@@ -24,26 +29,26 @@ def tile_temporalnmf_kernel(tc, table, w_in, w_age, b_in, age, w_hid, b_hid, off
     nc = tc.nc
     with (
         tc.tile_pool(name="held", bufs=1) as held,
-        tc.psum_pool(name="proj_banks", bufs=1) as proj_banks,
+        tc.psum_pool(name="banks", bufs=8) as banks,
     ):
+        age_strips = age.rearrange("t (r n) -> (t r) n", n=STRIP)
         table_quarters = table.rearrange("(q p i) e -> q p i e", p=P, i=FLIP)
         rows = held.tile([P, BLOCKS, E], BF16, name="rows")
-        for q in (0, 2, 1, 3):
-            queue = nc.sync if q * FLIP < HALF else nc.scalar
+        ages = held.tile([P, STRIP], F32, name="ages")
+        nc.gpsimd.memset(ages[QUADRANT : 2 * QUADRANT, :], 0.0)
+        for q in range(QUARTERS):
+            queue = nc.sync if q % 2 == 0 else nc.scalar
             queue.dma_start(rows[:, q * FLIP : (q + 1) * FLIP, :], table_quarters[q])
+        for quadrant in (0, 2, 3):
+            nc.sync.dma_start(ages[quadrant * QUADRANT : (quadrant + 1) * QUADRANT, :], age_strips)
+        offsets = held.tile([P, N // 16], U16, name="offsets")
+        nc.sync.dma_start(offsets[:], offs)
         w_age_col = held.tile([H, 1], F32, name="w_age_col")
         nc.sync.dma_start(w_age_col[:], w_age)
         b_in_col = held.tile([H, 1], F32, name="b_in_col")
         nc.sync.dma_start(b_in_col[:], b_in)
-        ages = [held.tile([P, N], F32, name=f"ages{t}") for t in range(D)]
-        for t in range(D // 2):
-            nc.sync.dma_start(ages[t][:], age[t, :].partition_broadcast(P))
-        offsets = held.tile([P, N // 16], U16, name="offsets")
-        nc.sync.dma_start(offsets[:], offs)
         w_in_sb = held.tile([E, H], BF16, name="w_in_sb")
         nc.sync.dma_start(w_in_sb[:], w_in)
-        for t in range(D // 2, D):
-            nc.sync.dma_start(ages[t][:], age[t, :].partition_broadcast(P))
         w_hid_sb = held.tile([H, H], BF16, name="w_hid_sb")
         nc.sync.dma_start(w_hid_sb[:], w_hid)
         b_hid_col = held.tile([H, 1], F32, name="b_hid_col")
@@ -51,103 +56,127 @@ def tile_temporalnmf_kernel(tc, table, w_in, w_age, b_in, age, w_hid, b_hid, off
 
         dummy = held.tile([P, 1], F32, name="dummy")
         nc.gpsimd.memset(dummy[:], 1.0)
-        nc.scalar.sqrt(dummy[:], dummy[:])
+        nc.scalar.activation(dummy[:], dummy[:], ACT.Abs_reciprocal_sqrt)
         identity = held.tile([P, P], BF16, name="identity")
         masks.make_identity(nc, identity[:])
+        pick_two = held.tile([P, QUADRANT], BF16, name="pick_two")
+        nc.gpsimd.tensor_tensor(pick_two[:], identity[:, :QUADRANT], identity[:, 2 * QUADRANT : 3 * QUADRANT], ADD)
+        pick = held.tile([P, QUADRANT], BF16, name="pick")
+        nc.gpsimd.tensor_tensor(pick[:], pick_two[:], identity[:, 3 * QUADRANT :], ADD)
+
         w_hid_minus = held.tile([H, H], BF16, name="w_hid_minus")
-        nc.gpsimd.tensor_scalar_mul(w_hid_minus[:], w_hid_sb[:], -1.0)
+        nc.gpsimd.tensor_scalar(w_hid_minus[:], w_hid_sb[:], -1.0, 1.0, op0=MULT, op1=MULT)
         b_hid_low = held.tile([H, 1], F32, name="b_hid_low")
-        nc.gpsimd.tensor_scalar_mul(b_hid_low[:], b_hid_col[:], SLOPE)
+        nc.gpsimd.tensor_scalar(b_hid_low[:], b_hid_col[:], SLOPE, 1.0, op0=MULT, op1=MULT)
 
         window = held.tile([E, S], BF16, name="window")
-        with (
-            tc.tile_pool(name="shrinking", bufs=1) as shrinking,
-            tc.psum_pool(name="flip_banks", bufs=1) as flip_banks,
-        ):
+        parts = held.tile([P, STRIP], BF16, name="parts")
+        with tc.tile_pool(name="shrinking", bufs=1) as shrinking:
             squares = shrinking.tile([P, BLOCKS, E], BF16, name="squares")
-            sumsq = shrinking.tile([P, BLOCKS], F32, name="sumsq")
-            for b in range(HALF):
-                nc.vector.scalar_tensor_tensor(
-                    out=squares[:, b, :],
-                    in0=rows[:, b, :],
-                    scalar=1.0,
-                    in1=rows[:, b, :],
-                    op0=MULT,
-                    op1=MULT,
-                    accum_out=sumsq[:, b : b + 1],
-                )
-            for b in range(HALF, BLOCKS):
-                nc.scalar.activation(squares[:, b, :], rows[:, b, :], ACT.Square, accum_out=sumsq[:, b : b + 1])
+            sumsq = [shrinking.tile([P, FLIP], F32, name=f"sumsq{q}") for q in range(QUARTERS)]
+            for b in range(BLOCKS):
+                block_sum = sumsq[b // FLIP][:, b % FLIP : b % FLIP + 1]
+                if b % 2 == 0:
+                    nc.vector.scalar_tensor_tensor(
+                        out=squares[:, b, :],
+                        in0=rows[:, b, :],
+                        scalar=1.0,
+                        in1=rows[:, b, :],
+                        op0=MULT,
+                        op1=MULT,
+                        accum_out=block_sum,
+                    )
+                else:
+                    nc.scalar.activation(squares[:, b, :], rows[:, b, :], ACT.Square, accum_out=block_sum)
 
-            norm = shrinking.tile([P, BLOCKS], F32, name="norm")
-            nc.scalar.sqrt(norm[:], sumsq[:])
-            divisor = shrinking.tile([P, BLOCKS], F32, name="divisor")
-            nc.vector.tensor_scalar(divisor[:], norm[:], EPS, 1.0, op0=ADD, op1=MAX)
-            factor = shrinking.tile([P, BLOCKS], F32, name="factor")
-            nc.vector.reciprocal(factor[:], divisor[:])
+            half, last = 2 * QUADRANT, 3 * QUADRANT
+            nc.scalar.activation(parts[:], ages[:], ACT.Relu)
+            clamped = shrinking.tile([P, STRIP], F32, name="clamped")
+            nc.scalar.activation(clamped[half:, :], ages[half:, :], ACT.Relu)
+            rest = shrinking.tile([P, STRIP], F32, name="rest")
+            nc.vector.tensor_tensor(rest[half:, :], clamped[half:, :], parts[half:, :], SUB)
+            nc.vector.tensor_copy(parts[half:, :], rest[half:, :])
+            nc.vector.tensor_tensor(parts[last:, :], rest[last:, :], parts[last:, :], SUB)
 
             embs_rows = shrinking.tile([P, BLOCKS, E], BF16, name="embs_rows")
-            flipped = [flip_banks.tile([E, PIECE], BF16, name=f"flipped{q}") for q in range(BLOCKS // FLIP)]
-            for i in range(HALF):
-                for b in (i, HALF + i):
-                    if b < HALF:
-                        nc.vector.tensor_scalar(embs_rows[:, b, :], rows[:, b, :], factor[:, b : b + 1], None, op0=MULT)
-                    else:
-                        nc.scalar.activation(embs_rows[:, b, :], rows[:, b, :], ACT.Copy, scale=factor[:, b : b + 1])
-                    nc.tensor.transpose(
-                        flipped[b // FLIP][:, (b % FLIP) * P : (b % FLIP + 1) * P], embs_rows[:, b, :], identity[:]
-                    )
-            for q in (0, 2, 1, 3):
+            for q in range(QUARTERS):
+                longest = shrinking.tile([P, FLIP], F32, name=f"longest{q}")
+                nc.vector.tensor_scalar(longest[:], sumsq[q][:], 2.0 * EPS, 1.0, op0=ADD, op1=MAX)
+                factor = shrinking.tile([P, FLIP], F32, name=f"factor{q}")
+                nc.scalar.activation(factor[:], longest[:], ACT.Abs_reciprocal_sqrt)
+                flipped = banks.tile([E, PIECE], BF16, name="flipped", tag="bank")
+                for i in range(FLIP):
+                    b = q * FLIP + i
+                    nc.vector.tensor_scalar(embs_rows[:, b, :], rows[:, b, :], factor[:, i : i + 1], None, op0=MULT)
+                    nc.tensor.transpose(flipped[:, i * P : (i + 1) * P], embs_rows[:, b, :], identity[:])
                 in_order = window[:, q * PIECE : (q + 1) * PIECE].rearrange("e (p i) -> e p i", i=FLIP)
-                by_block = flipped[q][:].rearrange("e (i p) -> e p i", i=FLIP)
-                if q * FLIP < HALF:
+                by_block = flipped[:].rearrange("e (i p) -> e p i", i=FLIP)
+                if q % 2 == 0:
                     nc.vector.tensor_copy(in_order, by_block)
                 else:
                     nc.scalar.copy(in_order, by_block)
 
-        proj = [proj_banks.tile([H, PIECE], F32, name=f"proj{g}") for g in range(PIECES)]
+        chunks = [(t, g) for t in range(D) for g in range(PIECES)]
+        on_all = []
+
+        def spread(t, g):
+            bank = banks.tile([H, PIECE], F32, name="bank")
+            for s in range(STRIPS):
+                r = (t * PIECES + g) * STRIPS + s
+                strip_picked = pick[:, r : r + 1].to_broadcast([P, H])
+                nc.tensor.matmul(bank[:, s * STRIP : (s + 1) * STRIP], strip_picked, parts[:], start=True, stop=True)
+            on_all.append(bank)
+
+        age_terms = []
+        for c in range(PIECES):
+            spread(*chunks[c])
+            age_term = held.tile([H, PIECE], F32, name=f"age_term{c}")
+            nc.scalar.activation(
+                age_term[:], on_all[c][:], ACT.Identity, bias=b_in_col[:, 0:1], scale=w_age_col[:, 0:1]
+            )
+            age_terms.append(age_term)
+
+        banked = []
         for g in range(PIECES):
+            looked_up = banks.tile([H, PIECE], F32, name="looked_up", tag="bank")
             piece = offsets[:, g * (PIECE // 16) : (g + 1) * (PIECE // 16)]
-            nc.tensor.matmul(proj[g][:], w_in_sb[:], window[:].indirect(piece), start=True, stop=True)
-
-        def weigh(t):
-            nc.vector.tensor_scalar(ages[t][:], ages[t][:], 0.0, w_age_col[:, 0:1], op0=MAX, op1=MULT)
-
-        weigh(0)
+            nc.tensor.matmul(looked_up[:], w_in_sb[:], window[:].indirect(piece), start=True, stop=True)
+            banked.append(looked_up)
+        for c in range(PIECES, AHEAD):
+            spread(*chunks[c])
 
         with (
             tc.tile_pool(name="work", bufs=4) as work,
-            tc.tile_pool(name="results", bufs=D * PIECES) as results,
-            tc.psum_pool(name="y_banks", bufs=LAG + 2) as y_banks,
+            tc.tile_pool(name="results", bufs=CHUNKS) as results,
         ):
-            chunks = [(t, g) for t in range(D) for g in range(PIECES)]
-            products = []
+            proj, products = [], []
 
-            def first_layer(t, g):
+            def first_layer(c):
                 z = work.tile([H, PIECE], F32, name="z")
-                nc.vector.scalar_tensor_tensor(
-                    out=z[:],
-                    in0=proj[g][:],
-                    scalar=b_in_col[:, 0:1],
-                    in1=ages[t][:, g * PIECE : (g + 1) * PIECE],
-                    op0=ADD,
-                    op1=ADD,
-                )
-                if g == 0 and t + 1 < D:
-                    weigh(t + 1)
+                g = chunks[c][1]
+                if c < PIECES:
+                    nc.vector.tensor_tensor(z[:], banked[g][:], age_terms[c][:], ADD)
+                    with_bias = held.tile([H, PIECE], F32, name=f"with_bias{g}")
+                    nc.scalar.activation(with_bias[:], banked[g][:], ACT.Identity, bias=b_in_col[:, 0:1])
+                    proj.append(with_bias)
+                else:
+                    nc.vector.scalar_tensor_tensor(
+                        out=z[:], in0=on_all[c][:], scalar=w_age_col[:, 0:1], in1=proj[g][:], op0=MULT, op1=ADD
+                    )
                 h_plus = work.tile([H, PIECE], BF16, name="h_plus")
                 nc.gpsimd.tensor_scalar(h_plus[:], z[:], FLT_MAX, 0.0, op0=MIN, op1=MAX)
                 h_minus = work.tile([H, PIECE], BF16, name="h_minus")
-                if len(products) % 4 == 3:
+                if c % 3 == 1:
                     nc.vector.tensor_scalar(h_minus[:], z[:], -SLOPE, 0.0, op0=MULT, op1=MAX)
                 else:
                     nc.scalar.activation(h_minus[:], z[:], ACT.Relu, scale=-SLOPE)
-                y = y_banks.tile([H, PIECE], F32, name="y")
+                y = banks.tile([H, PIECE], F32, name="y", tag="bank")
                 nc.tensor.matmul(y[:], w_hid_sb[:], h_plus[:], start=True, stop=False)
                 nc.tensor.matmul(y[:], w_hid_minus[:], h_minus[:], start=False, stop=True)
                 products.append(y)
 
             def second_layer(c):
+                t, g = chunks[c]
                 y = products[c]
                 low = work.tile([H, PIECE], F32, name="low")
                 nc.scalar.activation(low[:], y[:], ACT.Identity, bias=b_hid_low[:, 0:1], scale=SLOPE)
@@ -155,10 +184,12 @@ def tile_temporalnmf_kernel(tc, table, w_in, w_age, b_in, age, w_hid, b_hid, off
                 nc.vector.scalar_tensor_tensor(
                     out=result[:], in0=y[:], scalar=b_hid_col[:, 0:1], in1=low[:], op0=ADD, op1=MAX
                 )
-                nc.sync.dma_start(out[:, c * PIECE : (c + 1) * PIECE], result[:])
+                nc.sync.dma_start(out[:, t * N + g * PIECE : t * N + (g + 1) * PIECE], result[:])
 
-            for step in range(len(chunks) + LAG):
-                if step < len(chunks):
-                    first_layer(*chunks[step])
+            for step in range(CHUNKS + LAG):
+                if step + AHEAD < CHUNKS:
+                    spread(*chunks[step + AHEAD])
+                if step < CHUNKS:
+                    first_layer(step)
                 if step >= LAG:
                     second_layer(step - LAG)

@@ -15,7 +15,7 @@ BLOCKS = S // P
 QUARTERS = BLOCKS // FLIP
 STRIP = D * N // QUADRANT
 STRIPS = PIECE // STRIP
-LAG = 6
+LAG = 8
 AHEAD = 4
 FLT_MAX = 3.4028234663852886e38
 
@@ -41,6 +41,8 @@ def tile_temporalnmf_kernel(tc, table, w_in, w_age, b_in, age, w_hid, b_hid, off
             queue.dma_start(rows[:, q * FLIP : (q + 1) * FLIP, :], table_quarters[q])
         for quadrant in (0, 2, 3):
             nc.sync.dma_start(ages[quadrant * QUADRANT : (quadrant + 1) * QUADRANT, :], age_strips)
+        w_hid_sb = held.tile([H, H], BF16, name="w_hid_sb")
+        nc.sync.dma_start(w_hid_sb[:], w_hid)
         offsets = held.tile([P, N // 16], U16, name="offsets")
         nc.sync.dma_start(offsets[:], offs)
         w_age_col = held.tile([H, 1], F32, name="w_age_col")
@@ -49,45 +51,80 @@ def tile_temporalnmf_kernel(tc, table, w_in, w_age, b_in, age, w_hid, b_hid, off
         nc.sync.dma_start(b_in_col[:], b_in)
         w_in_sb = held.tile([E, H], BF16, name="w_in_sb")
         nc.sync.dma_start(w_in_sb[:], w_in)
-        w_hid_sb = held.tile([H, H], BF16, name="w_hid_sb")
-        nc.sync.dma_start(w_hid_sb[:], w_hid)
         b_hid_col = held.tile([H, 1], F32, name="b_hid_col")
         nc.sync.dma_start(b_hid_col[:], b_hid)
 
+        two_eps = held.tile([P, 1], F32, name="two_eps")
+        nc.gpsimd.memset(two_eps[:], 2.0 * EPS)
         dummy = held.tile([P, 1], F32, name="dummy")
-        nc.gpsimd.memset(dummy[:], 1.0)
-        nc.scalar.activation(dummy[:], dummy[:], ACT.Abs_reciprocal_sqrt)
+        nc.scalar.activation(dummy[:], two_eps[:], ACT.Abs_reciprocal_sqrt)
         identity = held.tile([P, P], BF16, name="identity")
         masks.make_identity(nc, identity[:])
         pick_two = held.tile([P, QUADRANT], BF16, name="pick_two")
         nc.gpsimd.tensor_tensor(pick_two[:], identity[:, :QUADRANT], identity[:, 2 * QUADRANT : 3 * QUADRANT], ADD)
         pick = held.tile([P, QUADRANT], BF16, name="pick")
         nc.gpsimd.tensor_tensor(pick[:], pick_two[:], identity[:, 3 * QUADRANT :], ADD)
-
-        w_hid_minus = held.tile([H, H], BF16, name="w_hid_minus")
-        nc.gpsimd.tensor_scalar(w_hid_minus[:], w_hid_sb[:], -1.0, 1.0, op0=MULT, op1=MULT)
-        b_hid_low = held.tile([H, 1], F32, name="b_hid_low")
-        nc.gpsimd.tensor_scalar(b_hid_low[:], b_hid_col[:], SLOPE, 1.0, op0=MULT, op1=MULT)
+        per_day = N // STRIP
+        turn = held.tile([P, D - 1, per_day], BF16, name="turn")
+        later_days = pick[:, per_day:].rearrange("p (t r) -> p t r", r=per_day)
+        nc.gpsimd.tensor_tensor(
+            turn[:], later_days, pick[:, :per_day].unsqueeze(1).to_broadcast([P, D - 1, per_day]), SUB
+        )
 
         window = held.tile([E, S], BF16, name="window")
         parts = held.tile([P, STRIP], BF16, name="parts")
         with tc.tile_pool(name="shrinking", bufs=1) as shrinking:
             squares = shrinking.tile([P, BLOCKS, E], BF16, name="squares")
             sumsq = [shrinking.tile([P, FLIP], F32, name=f"sumsq{q}") for q in range(QUARTERS)]
-            for b in range(BLOCKS):
-                block_sum = sumsq[b // FLIP][:, b % FLIP : b % FLIP + 1]
-                if b % 2 == 0:
-                    nc.vector.scalar_tensor_tensor(
-                        out=squares[:, b, :],
-                        in0=rows[:, b, :],
-                        scalar=1.0,
-                        in1=rows[:, b, :],
-                        op0=MULT,
-                        op1=MULT,
-                        accum_out=block_sum,
-                    )
-                else:
-                    nc.scalar.activation(squares[:, b, :], rows[:, b, :], ACT.Square, accum_out=block_sum)
+            embs_rows = shrinking.tile([P, BLOCKS, E], BF16, name="embs_rows")
+
+            def sum_squares(q):
+                for i in range(FLIP):
+                    b = q * FLIP + i
+                    if i % 2 == 0:
+                        nc.vector.scalar_tensor_tensor(
+                            out=squares[:, b, :],
+                            in0=rows[:, b, :],
+                            scalar=1.0,
+                            in1=rows[:, b, :],
+                            op0=MULT,
+                            op1=MULT,
+                            accum_out=sumsq[q][:, i : i + 1],
+                        )
+                    else:
+                        nc.scalar.activation(
+                            squares[:, b, :], rows[:, b, :], ACT.Square, accum_out=sumsq[q][:, i : i + 1]
+                        )
+
+            def shrink_and_flip(q):
+                inverse = shrinking.tile([P, FLIP], F32, name=f"inverse{q}")
+                nc.scalar.activation(inverse[:], sumsq[q][:], ACT.Abs_reciprocal_sqrt, bias=two_eps[:, 0:1])
+                factor = shrinking.tile([P, FLIP], F32, name=f"factor{q}")
+                nc.vector.tensor_scalar_min(factor[:], inverse[:], 1.0)
+                in_order = window[:, q * PIECE : (q + 1) * PIECE].rearrange("e (p i) -> e p i", i=FLIP)
+                shares = 2 if q == QUARTERS - 1 else 1
+                width = FLIP // shares
+                for share in range(shares):
+                    flipped = banks.tile([E, width * P], BF16, name="flipped", tag="bank")
+                    for i in range(width):
+                        n = share * width + i
+                        b = q * FLIP + n
+                        nc.vector.tensor_scalar(
+                            embs_rows[:, b, :], rows[:, b, :], factor[:, n : n + 1], None, op0=MULT
+                        )
+                        nc.tensor.transpose(flipped[:, i * P : (i + 1) * P], embs_rows[:, b, :], identity[:])
+                    neighbours = in_order[:, :, share * width : (share + 1) * width]
+                    by_block = flipped[:].rearrange("e (i p) -> e p i", i=width)
+                    if (q + share) % 2 == 0:
+                        nc.scalar.copy(neighbours, by_block)
+                    else:
+                        nc.vector.tensor_copy(neighbours, by_block)
+
+            sum_squares(0)
+            for q in range(QUARTERS):
+                if q + 1 < QUARTERS:
+                    sum_squares(q + 1)
+                shrink_and_flip(q)
 
             half, last = 2 * QUADRANT, 3 * QUADRANT
             nc.scalar.activation(parts[:], ages[:], ACT.Relu)
@@ -98,23 +135,10 @@ def tile_temporalnmf_kernel(tc, table, w_in, w_age, b_in, age, w_hid, b_hid, off
             nc.vector.tensor_copy(parts[half:, :], rest[half:, :])
             nc.vector.tensor_tensor(parts[last:, :], rest[last:, :], parts[last:, :], SUB)
 
-            embs_rows = shrinking.tile([P, BLOCKS, E], BF16, name="embs_rows")
-            for q in range(QUARTERS):
-                longest = shrinking.tile([P, FLIP], F32, name=f"longest{q}")
-                nc.vector.tensor_scalar(longest[:], sumsq[q][:], 2.0 * EPS, 1.0, op0=ADD, op1=MAX)
-                factor = shrinking.tile([P, FLIP], F32, name=f"factor{q}")
-                nc.scalar.activation(factor[:], longest[:], ACT.Abs_reciprocal_sqrt)
-                flipped = banks.tile([E, PIECE], BF16, name="flipped", tag="bank")
-                for i in range(FLIP):
-                    b = q * FLIP + i
-                    nc.vector.tensor_scalar(embs_rows[:, b, :], rows[:, b, :], factor[:, i : i + 1], None, op0=MULT)
-                    nc.tensor.transpose(flipped[:, i * P : (i + 1) * P], embs_rows[:, b, :], identity[:])
-                in_order = window[:, q * PIECE : (q + 1) * PIECE].rearrange("e (p i) -> e p i", i=FLIP)
-                by_block = flipped[:].rearrange("e (i p) -> e p i", i=FLIP)
-                if q % 2 == 0:
-                    nc.vector.tensor_copy(in_order, by_block)
-                else:
-                    nc.scalar.copy(in_order, by_block)
+        w_hid_minus = held.tile([H, H], BF16, name="w_hid_minus")
+        nc.gpsimd.tensor_scalar(w_hid_minus[:], w_hid_sb[:], -1.0, 1.0, op0=MULT, op1=MULT)
+        b_hid_low = held.tile([H, 1], F32, name="b_hid_low")
+        nc.gpsimd.tensor_scalar(b_hid_low[:], b_hid_col[:], SLOPE, 1.0, op0=MULT, op1=MULT)
 
         chunks = [(t, g) for t in range(D) for g in range(PIECES)]
         on_all = []
@@ -122,8 +146,9 @@ def tile_temporalnmf_kernel(tc, table, w_in, w_age, b_in, age, w_hid, b_hid, off
         def spread(t, g):
             bank = banks.tile([H, PIECE], F32, name="bank")
             for s in range(STRIPS):
-                r = (t * PIECES + g) * STRIPS + s
-                strip_picked = pick[:, r : r + 1].to_broadcast([P, H])
+                r = g * STRIPS + s
+                column = pick[:, r : r + 1] if t == 0 else turn[:, t - 1, r : r + 1]
+                strip_picked = column.to_broadcast([P, H])
                 nc.tensor.matmul(bank[:, s * STRIP : (s + 1) * STRIP], strip_picked, parts[:], start=True, stop=True)
             on_all.append(bank)
 
@@ -146,27 +171,28 @@ def tile_temporalnmf_kernel(tc, table, w_in, w_age, b_in, age, w_hid, b_hid, off
             spread(*chunks[c])
 
         with (
-            tc.tile_pool(name="work", bufs=4) as work,
+            tc.tile_pool(name="work", bufs=8) as work,
             tc.tile_pool(name="results", bufs=CHUNKS) as results,
         ):
-            proj, products = [], []
+            first_day, products = [], []
+            for g in range(PIECES):
+                z = held.tile([H, PIECE], F32, name=f"first_day{g}")
+                nc.vector.tensor_tensor(z[:], banked[g][:], age_terms[g][:], ADD)
+                first_day.append(z)
 
             def first_layer(c):
-                z = work.tile([H, PIECE], F32, name="z")
-                g = chunks[c][1]
-                if c < PIECES:
-                    nc.vector.tensor_tensor(z[:], banked[g][:], age_terms[c][:], ADD)
-                    with_bias = held.tile([H, PIECE], F32, name=f"with_bias{g}")
-                    nc.scalar.activation(with_bias[:], banked[g][:], ACT.Identity, bias=b_in_col[:, 0:1])
-                    proj.append(with_bias)
+                t, g = chunks[c]
+                if t == 0:
+                    z = first_day[g]
                 else:
+                    z = work.tile([H, PIECE], F32, name="z")
                     nc.vector.scalar_tensor_tensor(
-                        out=z[:], in0=on_all[c][:], scalar=w_age_col[:, 0:1], in1=proj[g][:], op0=MULT, op1=ADD
+                        out=z[:], in0=on_all[c][:], scalar=w_age_col[:, 0:1], in1=first_day[g][:], op0=MULT, op1=ADD
                     )
                 h_plus = work.tile([H, PIECE], BF16, name="h_plus")
                 nc.gpsimd.tensor_scalar(h_plus[:], z[:], FLT_MAX, 0.0, op0=MIN, op1=MAX)
                 h_minus = work.tile([H, PIECE], BF16, name="h_minus")
-                if c % 3 == 1:
+                if c >= CHUNKS - 2:
                     nc.vector.tensor_scalar(h_minus[:], z[:], -SLOPE, 0.0, op0=MULT, op1=MAX)
                 else:
                     nc.scalar.activation(h_minus[:], z[:], ACT.Relu, scale=-SLOPE)

@@ -9,7 +9,6 @@ P = 128
 QUADRANT = 32
 PIECE = 512
 PIECES = N // PIECE
-CHUNKS = D * PIECES
 FLIP = PIECE // P
 BLOCKS = S // P
 QUARTERS = BLOCKS // FLIP
@@ -140,8 +139,12 @@ def tile_temporalnmf_kernel(tc, table, w_in, w_age, b_in, age, w_hid, b_hid, off
         b_hid_low = held.tile([H, 1], F32, name="b_hid_low")
         nc.gpsimd.tensor_scalar(b_hid_low[:], b_hid_col[:], SLOPE, 1.0, op0=MULT, op1=MULT)
 
-        chunks = [(t, g) for t in range(D) for g in range(PIECES)]
-        on_all = []
+        pieces = [(t, g) for t in range(D) for g in range(PIECES)]
+        chunks = []
+        for t, g in pieces:
+            width = PIECE // 2 if (t, g) in (pieces[0], pieces[-1]) else PIECE
+            chunks += [(t, g, start, width) for start in range(0, PIECE, width)]
+        on_all = {}
 
         def spread(t, g):
             bank = banks.tile([H, PIECE], F32, name="bank")
@@ -150,72 +153,83 @@ def tile_temporalnmf_kernel(tc, table, w_in, w_age, b_in, age, w_hid, b_hid, off
                 column = pick[:, r : r + 1] if t == 0 else turn[:, t - 1, r : r + 1]
                 strip_picked = column.to_broadcast([P, H])
                 nc.tensor.matmul(bank[:, s * STRIP : (s + 1) * STRIP], strip_picked, parts[:], start=True, stop=True)
-            on_all.append(bank)
+            on_all[t, g] = bank
 
         age_terms = []
-        for c in range(PIECES):
-            spread(*chunks[c])
-            age_term = held.tile([H, PIECE], F32, name=f"age_term{c}")
+        for g in range(PIECES):
+            spread(0, g)
+            age_term = held.tile([H, PIECE], F32, name=f"age_term{g}")
             nc.scalar.activation(
-                age_term[:], on_all[c][:], ACT.Identity, bias=b_in_col[:, 0:1], scale=w_age_col[:, 0:1]
+                age_term[:], on_all[0, g][:], ACT.Identity, bias=b_in_col[:, 0:1], scale=w_age_col[:, 0:1]
             )
             age_terms.append(age_term)
 
-        banked = []
-        for g in range(PIECES):
-            looked_up = banks.tile([H, PIECE], F32, name="looked_up", tag="bank")
-            piece = offsets[:, g * (PIECE // 16) : (g + 1) * (PIECE // 16)]
-            nc.tensor.matmul(looked_up[:], w_in_sb[:], window[:].indirect(piece), start=True, stop=True)
-            banked.append(looked_up)
-        for c in range(PIECES, AHEAD):
-            spread(*chunks[c])
+        banked = {}
+        for t, g, start, width in chunks:
+            if t == 0:
+                looked_up = banks.tile([H, width], F32, name="looked_up", tag="bank")
+                first = g * PIECE + start
+                listed = offsets[:, first // 16 : (first + width) // 16]
+                nc.tensor.matmul(looked_up[:], w_in_sb[:], window[:].indirect(listed), start=True, stop=True)
+                banked[g, start] = looked_up
+        for t, g in pieces[PIECES:AHEAD]:
+            spread(t, g)
 
+        first_day = held.tile([H, N], F32, name="first_day")
         with (
             tc.tile_pool(name="work", bufs=8) as work,
-            tc.tile_pool(name="results", bufs=CHUNKS) as results,
+            tc.tile_pool(name="results", bufs=len(chunks)) as results,
         ):
-            first_day, products = [], []
-            for g in range(PIECES):
-                z = held.tile([H, PIECE], F32, name=f"first_day{g}")
-                nc.vector.tensor_tensor(z[:], banked[g][:], age_terms[g][:], ADD)
-                first_day.append(z)
+            products = []
 
             def first_layer(c):
-                t, g = chunks[c]
+                t, g, start, width = chunks[c]
+                columns = slice(start, start + width)
+                of_first_day = first_day[:, g * PIECE + start : g * PIECE + start + width]
                 if t == 0:
-                    z = first_day[g]
+                    z = of_first_day
+                    nc.vector.tensor_tensor(z, banked[g, start][:], age_terms[g][:, columns], ADD)
                 else:
-                    z = work.tile([H, PIECE], F32, name="z")
+                    later = work.tile([H, width], F32, name="later")
+                    z = later[:]
                     nc.vector.scalar_tensor_tensor(
-                        out=z[:], in0=on_all[c][:], scalar=w_age_col[:, 0:1], in1=first_day[g][:], op0=MULT, op1=ADD
+                        out=z,
+                        in0=on_all[t, g][:, columns],
+                        scalar=w_age_col[:, 0:1],
+                        in1=of_first_day,
+                        op0=MULT,
+                        op1=ADD,
                     )
-                h_plus = work.tile([H, PIECE], BF16, name="h_plus")
-                nc.gpsimd.tensor_scalar(h_plus[:], z[:], FLT_MAX, 0.0, op0=MIN, op1=MAX)
-                h_minus = work.tile([H, PIECE], BF16, name="h_minus")
-                if c >= CHUNKS - 2:
-                    nc.vector.tensor_scalar(h_minus[:], z[:], -SLOPE, 0.0, op0=MULT, op1=MAX)
+                h_plus = work.tile([H, width], BF16, name="h_plus")
+                nc.gpsimd.tensor_scalar(h_plus[:], z, FLT_MAX, 0.0, op0=MIN, op1=MAX)
+                h_minus = work.tile([H, width], BF16, name="h_minus")
+                if c >= len(chunks) - 3:
+                    nc.vector.tensor_scalar(h_minus[:], z, -SLOPE, 0.0, op0=MULT, op1=MAX)
                 else:
-                    nc.scalar.activation(h_minus[:], z[:], ACT.Relu, scale=-SLOPE)
-                y = banks.tile([H, PIECE], F32, name="y", tag="bank")
+                    nc.scalar.activation(h_minus[:], z, ACT.Relu, scale=-SLOPE)
+                y = banks.tile([H, width], F32, name="y", tag="bank")
                 nc.tensor.matmul(y[:], w_hid_sb[:], h_plus[:], start=True, stop=False)
                 nc.tensor.matmul(y[:], w_hid_minus[:], h_minus[:], start=False, stop=True)
                 products.append(y)
 
             def second_layer(c):
-                t, g = chunks[c]
+                t, g, start, width = chunks[c]
                 y = products[c]
-                low = work.tile([H, PIECE], F32, name="low")
+                low = work.tile([H, width], F32, name="low")
                 nc.scalar.activation(low[:], y[:], ACT.Identity, bias=b_hid_low[:, 0:1], scale=SLOPE)
-                result = results.tile([H, PIECE], F32, name="result")
+                result = results.tile([H, width], F32, name="result")
                 nc.vector.scalar_tensor_tensor(
                     out=result[:], in0=y[:], scalar=b_hid_col[:, 0:1], in1=low[:], op0=ADD, op1=MAX
                 )
-                nc.sync.dma_start(out[:, t * N + g * PIECE : t * N + (g + 1) * PIECE], result[:])
+                first = t * N + g * PIECE + start
+                nc.sync.dma_start(out[:, first : first + width], result[:])
 
-            for step in range(CHUNKS + LAG):
-                if step + AHEAD < CHUNKS:
-                    spread(*chunks[step + AHEAD])
-                if step < CHUNKS:
+            for step in range(len(chunks) + LAG):
+                if step < len(chunks):
+                    t, g, start, width = chunks[step]
+                    ahead = t * PIECES + g + AHEAD
+                    if start == 0 and ahead < len(pieces):
+                        spread(*pieces[ahead])
                     first_layer(step)
                 if step >= LAG:
                     second_layer(step - LAG)

@@ -100,24 +100,29 @@ def tile_temporalnmf_kernel(tc, table, w_in, w_age, b_in, age, w_hid, b_hid, off
                 nc.scalar.activation(inverse[:], sumsq[q][:], ACT.Abs_reciprocal_sqrt, bias=two_eps[:, 0:1])
                 factor = shrinking.tile([P, FLIP], F32, name=f"factor{q}")
                 nc.vector.tensor_scalar_min(factor[:], inverse[:], 1.0)
-                in_order = window[:, q * PIECE : (q + 1) * PIECE].rearrange("e (p i) -> e p i", i=FLIP)
                 shares = 2 if q == QUARTERS - 1 else 1
-                width = FLIP // shares
                 for share in range(shares):
-                    flipped = banks.tile([E, width * P], BF16, name="flipped", tag="bank")
-                    for i in range(width):
-                        n = share * width + i
-                        b = q * FLIP + n
-                        nc.vector.tensor_scalar(
-                            embs_rows[:, b, :], rows[:, b, :], factor[:, n : n + 1], None, op0=MULT
+                    width = P // shares
+                    flipped = banks.tile([E, width * FLIP], F32, name="flipped", tag="bank")
+                    by_neighbour = flipped[:].rearrange("e (p i) -> e i p", i=FLIP)
+                    for i in range(FLIP):
+                        b = q * FLIP + i
+                        if share == 0:
+                            nc.vector.tensor_scalar(
+                                embs_rows[:, b, :], rows[:, b, :], factor[:, i : i + 1], None, op0=MULT
+                            )
+                        nc.tensor.matmul(
+                            by_neighbour[:, i, :],
+                            embs_rows[:, b, :],
+                            identity[:, share * width : (share + 1) * width],
+                            start=True,
+                            stop=True,
                         )
-                        nc.tensor.transpose(flipped[:, i * P : (i + 1) * P], embs_rows[:, b, :], identity[:])
-                    neighbours = in_order[:, :, share * width : (share + 1) * width]
-                    by_block = flipped[:].rearrange("e (i p) -> e p i", i=width)
+                    first = q * PIECE + share * width * FLIP
                     if (q + share) % 2 == 0:
-                        nc.scalar.copy(neighbours, by_block)
+                        nc.scalar.copy(window[:, first : first + width * FLIP], flipped[:])
                     else:
-                        nc.vector.tensor_copy(neighbours, by_block)
+                        nc.vector.tensor_copy(window[:, first : first + width * FLIP], flipped[:])
 
             sum_squares(0)
             for q in range(QUARTERS):

@@ -14,8 +14,8 @@ BLOCKS = S // P
 QUARTERS = BLOCKS // FLIP
 STRIP = D * N // QUADRANT
 STRIPS = PIECE // STRIP
-LAG = 8
 AHEAD = 4
+LAG = 3
 FLT_MAX = 3.4028234663852886e38
 
 BF16, F32, U16 = mybir.dt.bfloat16, mybir.dt.float32, mybir.dt.uint16
@@ -145,10 +145,14 @@ def tile_temporalnmf_kernel(tc, table, w_in, w_age, b_in, age, w_hid, b_hid, off
         nc.gpsimd.tensor_scalar(b_hid_low[:], b_hid_col[:], SLOPE, 1.0, op0=MULT, op1=MULT)
 
         pieces = [(t, g) for t in range(D) for g in range(PIECES)]
-        chunks = []
-        for t, g in pieces:
-            width = PIECE // 2 if (t, g) in (pieces[0], pieces[-1]) else PIECE
-            chunks += [(t, g, start, width) for start in range(0, PIECE, width)]
+        groups = []
+        for t in range(D):
+            chunks_of_day = []
+            for g in range(PIECES):
+                width = PIECE // 2 if t == 0 or (t, g) == pieces[-1] else PIECE
+                chunks_of_day += [(t, first, width) for first in range(g * PIECE, (g + 1) * PIECE, width)]
+            groups += [[chunk] for chunk in chunks_of_day] if t in (0, D - 1) else [chunks_of_day]
+        chunks = [chunk for group in groups for chunk in group]
         on_all = {}
 
         def spread(t, g):
@@ -170,13 +174,12 @@ def tile_temporalnmf_kernel(tc, table, w_in, w_age, b_in, age, w_hid, b_hid, off
             age_terms.append(age_term)
 
         banked = {}
-        for t, g, start, width in chunks:
+        for t, first, width in chunks:
             if t == 0:
                 looked_up = banks.tile([H, width], F32, name="looked_up", tag="bank")
-                first = g * PIECE + start
                 listed = offsets[:, first // 16 : (first + width) // 16]
                 nc.tensor.matmul(looked_up[:], w_in_sb[:], window[:].indirect(listed), start=True, stop=True)
-                banked[g, start] = looked_up
+                banked[first] = looked_up
         for t, g in pieces[PIECES:AHEAD]:
             spread(t, g)
 
@@ -185,56 +188,62 @@ def tile_temporalnmf_kernel(tc, table, w_in, w_age, b_in, age, w_hid, b_hid, off
             tc.tile_pool(name="work", bufs=8) as work,
             tc.tile_pool(name="results", bufs=len(chunks)) as results,
         ):
-            products = []
+            products = {}
 
-            def first_layer(c):
-                t, g, start, width = chunks[c]
-                columns = slice(start, start + width)
-                of_first_day = first_day[:, g * PIECE + start : g * PIECE + start + width]
-                if t == 0:
-                    z = of_first_day
-                    nc.vector.tensor_tensor(z, banked[g, start][:], age_terms[g][:, columns], ADD)
+            def first_layer(group):
+                day, group_start = group[0][0], group[0][1]
+                group_width = sum(width for t, first, width in group)
+                if day == 0:
+                    z = first_day[:, group_start : group_start + group_width]
                 else:
-                    later = work.tile([H, width], F32, name="later")
+                    later = work.tile([H, group_width], F32, name="later")
                     z = later[:]
-                    nc.vector.scalar_tensor_tensor(
-                        out=z,
-                        in0=on_all[t, g][:, columns],
-                        scalar=w_age_col[:, 0:1],
-                        in1=of_first_day,
-                        op0=MULT,
-                        op1=ADD,
-                    )
-                h_plus = work.tile([H, width], BF16, name="h_plus")
+                for t, first, width in group:
+                    g = first // PIECE
+                    in_piece = slice(first - g * PIECE, first - g * PIECE + width)
+                    in_group = slice(first - group_start, first - group_start + width)
+                    if day == 0:
+                        nc.vector.tensor_tensor(z[:, in_group], banked[first][:], age_terms[g][:, in_piece], ADD)
+                    else:
+                        nc.vector.scalar_tensor_tensor(
+                            out=z[:, in_group],
+                            in0=on_all[t, g][:, in_piece],
+                            scalar=w_age_col[:, 0:1],
+                            in1=first_day[:, first : first + width],
+                            op0=MULT,
+                            op1=ADD,
+                        )
+                h_plus = work.tile([H, group_width], BF16, name="h_plus")
                 nc.gpsimd.tensor_scalar(h_plus[:], z, FLT_MAX, 0.0, op0=MIN, op1=MAX)
-                h_minus = work.tile([H, width], BF16, name="h_minus")
-                if c >= len(chunks) - 3:
-                    nc.vector.tensor_scalar(h_minus[:], z, -SLOPE, 0.0, op0=MULT, op1=MAX)
-                else:
-                    nc.scalar.activation(h_minus[:], z, ACT.Relu, scale=-SLOPE)
-                y = banks.tile([H, width], F32, name="y", tag="bank")
-                nc.tensor.matmul(y[:], w_hid_sb[:], h_plus[:], start=True, stop=False)
-                nc.tensor.matmul(y[:], w_hid_minus[:], h_minus[:], start=False, stop=True)
-                products.append(y)
+                for t, first, width in group:
+                    in_group = slice(first - group_start, first - group_start + width)
+                    h_minus = work.tile([H, width], BF16, name="h_minus")
+                    if t == D - 1:
+                        nc.vector.tensor_scalar(h_minus[:], z[:, in_group], -SLOPE, 0.0, op0=MULT, op1=MAX)
+                    else:
+                        nc.scalar.activation(h_minus[:], z[:, in_group], ACT.Relu, scale=-SLOPE)
+                    y = banks.tile([H, width], F32, name="y", tag="bank")
+                    nc.tensor.matmul(y[:], w_hid_sb[:], h_plus[:, in_group], start=True, stop=False)
+                    nc.tensor.matmul(y[:], w_hid_minus[:], h_minus[:], start=False, stop=True)
+                    products[t, first] = y
 
-            def second_layer(c):
-                t, g, start, width = chunks[c]
-                y = products[c]
+            def second_layer(t, first, width):
+                y = products[t, first]
                 low = work.tile([H, width], F32, name="low")
                 nc.scalar.activation(low[:], y[:], ACT.Identity, bias=b_hid_low[:, 0:1], scale=SLOPE)
                 result = results.tile([H, width], F32, name="result")
                 nc.vector.scalar_tensor_tensor(
                     out=result[:], in0=y[:], scalar=b_hid_col[:, 0:1], in1=low[:], op0=ADD, op1=MAX
                 )
-                first = t * N + g * PIECE + start
-                nc.sync.dma_start(out[:, first : first + width], result[:])
+                nc.sync.dma_start(out[:, t * N + first : t * N + first + width], result[:])
 
-            for step in range(len(chunks) + LAG):
-                if step < len(chunks):
-                    t, g, start, width = chunks[step]
-                    ahead = t * PIECES + g + AHEAD
-                    if start == 0 and ahead < len(pieces):
-                        spread(*pieces[ahead])
-                    first_layer(step)
+            for step in range(len(groups) + LAG):
+                if step < len(groups):
+                    for t, first, width in groups[step]:
+                        piece_ahead = t * PIECES + first // PIECE + AHEAD
+                        if first % PIECE == 0 and piece_ahead < len(pieces):
+                            spread(*pieces[piece_ahead])
+                    first_layer(groups[step])
                 if step >= LAG:
-                    second_layer(step - LAG)
+                    for chunk in groups[step - LAG]:
+                        second_layer(*chunk)

@@ -218,10 +218,7 @@ def tile_temporalnmf_kernel(tc, table, w_in, w_age, b_in, age, w_hid, b_hid, off
                 for t, first, width in group:
                     in_group = slice(first - group_start, first - group_start + width)
                     h_minus = work.tile([H, width], BF16, name="h_minus")
-                    if t == D - 1:
-                        nc.vector.tensor_scalar(h_minus[:], z[:, in_group], -SLOPE, 0.0, op0=MULT, op1=MAX)
-                    else:
-                        nc.scalar.activation(h_minus[:], z[:, in_group], ACT.Relu, scale=-SLOPE)
+                    nc.scalar.activation(h_minus[:], z[:, in_group], ACT.Relu, scale=-SLOPE)
                     y = banks.tile([H, width], F32, name="y", tag="bank")
                     nc.tensor.matmul(y[:], w_hid_sb[:], h_plus[:, in_group], start=True, stop=False)
                     nc.tensor.matmul(y[:], w_hid_minus[:], h_minus[:], start=False, stop=True)

@@ -227,7 +227,10 @@ def tile_temporalnmf_kernel(tc, table, w_in, w_age, b_in, age, w_hid, b_hid, off
             def second_layer(t, first, width):
                 y = products[t, first]
                 low = work.tile([H, width], F32, name="low")
-                nc.scalar.activation(low[:], y[:], ACT.Identity, bias=b_hid_low[:, 0:1], scale=SLOPE)
+                if (t, first) == (1, 0):
+                    nc.vector.tensor_scalar(low[:], y[:], SLOPE, b_hid_low[:, 0:1], op0=MULT, op1=ADD)
+                else:
+                    nc.scalar.activation(low[:], y[:], ACT.Identity, bias=b_hid_low[:, 0:1], scale=SLOPE)
                 result = results.tile([H, width], F32, name="result")
                 nc.vector.scalar_tensor_tensor(
                     out=result[:], in0=y[:], scalar=b_hid_col[:, 0:1], in1=low[:], op0=ADD, op1=MAX

import concourse.masks as masks
import concourse.mybir as mybir

S, E, H, D, N = 2048, 128, 128, 4, 1024
SLOPE, EPS = 0.3, 1e-7
FLOPS = 2 * E * H * N + 2 * H * H * D * N

P = 128
QUADRANT = 32
PIECE = 512
PIECES = N // PIECE
FLIP = PIECE // P
BLOCKS = S // P
QUARTERS = BLOCKS // FLIP
STRIP = D * N // QUADRANT
STRIPS = PIECE // STRIP
AHEAD = 4
LAG = 3
FLT_MAX = 3.4028234663852886e38

BF16, F32, U16 = mybir.dt.bfloat16, mybir.dt.float32, mybir.dt.uint16
ADD, MULT, SUB = mybir.AluOpType.add, mybir.AluOpType.mult, mybir.AluOpType.subtract
MAX, MIN = mybir.AluOpType.max, mybir.AluOpType.min
ACT = mybir.ActivationFunctionType


def tile_temporalnmf_kernel(tc, table, w_in, w_age, b_in, age, w_hid, b_hid, offs, out):
    nc = tc.nc
    with (
        tc.tile_pool(name="held", bufs=1) as held,
        tc.psum_pool(name="banks", bufs=8) as banks,
    ):
        age_strips = age.rearrange("t (r n) -> (t r) n", n=STRIP)
        table_quarters = table.rearrange("(q p i) e -> q p i e", p=P, i=FLIP)
        rows = held.tile([P, BLOCKS, E], BF16, name="rows")
        ages = held.tile([P, STRIP], F32, name="ages")
        nc.gpsimd.memset(ages[QUADRANT : 2 * QUADRANT, :], 0.0)
        for q in range(QUARTERS):
            queue = nc.sync if q % 2 == 0 else nc.scalar
            queue.dma_start(rows[:, q * FLIP : (q + 1) * FLIP, :], table_quarters[q])
        for quadrant in (0, 2, 3):
            nc.sync.dma_start(ages[quadrant * QUADRANT : (quadrant + 1) * QUADRANT, :], age_strips)
        w_hid_sb = held.tile([H, H], BF16, name="w_hid_sb")
        nc.sync.dma_start(w_hid_sb[:], w_hid)
        offsets = held.tile([P, N // 16], U16, name="offsets")
        nc.sync.dma_start(offsets[:], offs)
        w_age_col = held.tile([H, 1], F32, name="w_age_col")
        nc.sync.dma_start(w_age_col[:], w_age)
        b_in_col = held.tile([H, 1], F32, name="b_in_col")
        nc.sync.dma_start(b_in_col[:], b_in)
        w_in_sb = held.tile([E, H], BF16, name="w_in_sb")
        nc.sync.dma_start(w_in_sb[:], w_in)
        b_hid_col = held.tile([H, 1], F32, name="b_hid_col")
        nc.sync.dma_start(b_hid_col[:], b_hid)

        two_eps = held.tile([P, 1], F32, name="two_eps")
        nc.gpsimd.memset(two_eps[:], 2.0 * EPS)
        dummy = held.tile([P, 1], F32, name="dummy")
        nc.scalar.activation(dummy[:], two_eps[:], ACT.Abs_reciprocal_sqrt)
        identity = held.tile([P, P], BF16, name="identity")
        masks.make_identity(nc, identity[:])
        pick_two = held.tile([P, QUADRANT], BF16, name="pick_two")
        nc.gpsimd.tensor_tensor(pick_two[:], identity[:, :QUADRANT], identity[:, 2 * QUADRANT : 3 * QUADRANT], ADD)
        pick = held.tile([P, QUADRANT], BF16, name="pick")
        nc.gpsimd.tensor_tensor(pick[:], pick_two[:], identity[:, 3 * QUADRANT :], ADD)
        per_day = N // STRIP
        turn = held.tile([P, D - 1, per_day], BF16, name="turn")
        later_days = pick[:, per_day:].rearrange("p (t r) -> p t r", r=per_day)
        nc.gpsimd.tensor_tensor(
            turn[:], later_days, pick[:, :per_day].unsqueeze(1).to_broadcast([P, D - 1, per_day]), SUB
        )

        window = held.tile([E, S], BF16, name="window")
        parts = held.tile([P, STRIP], BF16, name="parts")
        with tc.tile_pool(name="shrinking", bufs=1) as shrinking:
            squares = shrinking.tile([P, BLOCKS, E], BF16, name="squares")
            sumsq = [shrinking.tile([P, FLIP], F32, name=f"sumsq{q}") for q in range(QUARTERS)]
            embs_rows = shrinking.tile([P, BLOCKS, E], BF16, name="embs_rows")

            def sum_squares(q):
                for i in range(FLIP):
                    b = q * FLIP + i
                    if i % 2 == 0:
                        nc.vector.scalar_tensor_tensor(
                            out=squares[:, b, :],
                            in0=rows[:, b, :],
                            scalar=1.0,
                            in1=rows[:, b, :],
                            op0=MULT,
                            op1=MULT,
                            accum_out=sumsq[q][:, i : i + 1],
                        )
                    else:
                        nc.scalar.activation(
                            squares[:, b, :], rows[:, b, :], ACT.Square, accum_out=sumsq[q][:, i : i + 1]
                        )

            def shrink_and_flip(q):
                inverse = shrinking.tile([P, FLIP], F32, name=f"inverse{q}")
                nc.scalar.activation(inverse[:], sumsq[q][:], ACT.Abs_reciprocal_sqrt, bias=two_eps[:, 0:1])
                factor = shrinking.tile([P, FLIP], F32, name=f"factor{q}")
                nc.vector.tensor_scalar_min(factor[:], inverse[:], 1.0)
                shares = 2 if q == QUARTERS - 1 else 1
                for share in range(shares):
                    width = P // shares
                    flipped = banks.tile([E, width * FLIP], F32, name="flipped", tag="bank")
                    by_neighbour = flipped[:].rearrange("e (p i) -> e i p", i=FLIP)
                    for i in range(FLIP):
                        b = q * FLIP + i
                        if share == 0:
                            nc.vector.tensor_scalar(
                                embs_rows[:, b, :], rows[:, b, :], factor[:, i : i + 1], None, op0=MULT
                            )
                        nc.tensor.matmul(
                            by_neighbour[:, i, :],
                            embs_rows[:, b, :],
                            identity[:, share * width : (share + 1) * width],
                            start=True,
                            stop=True,
                        )
                    first = q * PIECE + share * width * FLIP
                    if (q + share) % 2 == 0:
                        nc.scalar.copy(window[:, first : first + width * FLIP], flipped[:])
                    else:
                        nc.vector.tensor_copy(window[:, first : first + width * FLIP], flipped[:])

            sum_squares(0)
            for q in range(QUARTERS):
                if q + 1 < QUARTERS:
                    sum_squares(q + 1)
                shrink_and_flip(q)

            half, last = 2 * QUADRANT, 3 * QUADRANT
            nc.scalar.activation(parts[:], ages[:], ACT.Relu)
            clamped = shrinking.tile([P, STRIP], F32, name="clamped")
            nc.scalar.activation(clamped[half:, :], ages[half:, :], ACT.Relu)
            rest = shrinking.tile([P, STRIP], F32, name="rest")
            nc.vector.tensor_tensor(rest[half:, :], clamped[half:, :], parts[half:, :], SUB)
            nc.vector.tensor_copy(parts[half:, :], rest[half:, :])
            nc.vector.tensor_tensor(parts[last:, :], rest[last:, :], parts[last:, :], SUB)

        w_hid_minus = held.tile([H, H], BF16, name="w_hid_minus")
        nc.gpsimd.tensor_scalar(w_hid_minus[:], w_hid_sb[:], -1.0, 1.0, op0=MULT, op1=MULT)
        b_hid_low = held.tile([H, 1], F32, name="b_hid_low")
        nc.gpsimd.tensor_scalar(b_hid_low[:], b_hid_col[:], SLOPE, 1.0, op0=MULT, op1=MULT)

        pieces = [(t, g) for t in range(D) for g in range(PIECES)]
        groups = []
        for t in range(D):
            chunks_of_day = []
            for g in range(PIECES):
                width = PIECE // 2 if t == 0 or (t, g) == pieces[-1] else PIECE
                chunks_of_day += [(t, first, width) for first in range(g * PIECE, (g + 1) * PIECE, width)]
            groups += [[chunk] for chunk in chunks_of_day] if t in (0, D - 1) else [chunks_of_day]
        chunks = [chunk for group in groups for chunk in group]
        on_all = {}

        def spread(t, g):
            bank = banks.tile([H, PIECE], F32, name="bank")
            for s in range(STRIPS):
                r = g * STRIPS + s
                column = pick[:, r : r + 1] if t == 0 else turn[:, t - 1, r : r + 1]
                strip_picked = column.to_broadcast([P, H])
                nc.tensor.matmul(bank[:, s * STRIP : (s + 1) * STRIP], strip_picked, parts[:], start=True, stop=True)
            on_all[t, g] = bank

        age_terms = []
        for g in range(PIECES):
            spread(0, g)
            age_term = held.tile([H, PIECE], F32, name=f"age_term{g}")
            nc.scalar.activation(
                age_term[:], on_all[0, g][:], ACT.Identity, bias=b_in_col[:, 0:1], scale=w_age_col[:, 0:1]
            )
            age_terms.append(age_term)

        banked = {}
        for t, first, width in chunks:
            if t == 0:
                looked_up = banks.tile([H, width], F32, name="looked_up", tag="bank")
                listed = offsets[:, first // 16 : (first + width) // 16]
                nc.tensor.matmul(looked_up[:], w_in_sb[:], window[:].indirect(listed), start=True, stop=True)
                banked[first] = looked_up
        for t, g in pieces[PIECES:AHEAD]:
            spread(t, g)

        first_day = held.tile([H, N], F32, name="first_day")
        with (
            tc.tile_pool(name="work", bufs=8) as work,
            tc.tile_pool(name="results", bufs=len(chunks)) as results,
        ):
            products = {}

            def first_layer(group):
                day, group_start = group[0][0], group[0][1]
                group_width = sum(width for t, first, width in group)
                if day == 0:
                    z = first_day[:, group_start : group_start + group_width]
                else:
                    later = work.tile([H, group_width], F32, name="later")
                    z = later[:]
                for t, first, width in group:
                    g = first // PIECE
                    in_piece = slice(first - g * PIECE, first - g * PIECE + width)
                    in_group = slice(first - group_start, first - group_start + width)
                    if day == 0:
                        nc.vector.tensor_tensor(z[:, in_group], banked[first][:], age_terms[g][:, in_piece], ADD)
                    else:
                        nc.vector.scalar_tensor_tensor(
                            out=z[:, in_group],
                            in0=on_all[t, g][:, in_piece],
                            scalar=w_age_col[:, 0:1],
                            in1=first_day[:, first : first + width],
                            op0=MULT,
                            op1=ADD,
                        )
                h_plus = work.tile([H, group_width], BF16, name="h_plus")
                nc.gpsimd.tensor_scalar(h_plus[:], z, FLT_MAX, 0.0, op0=MIN, op1=MAX)
                for t, first, width in group:
                    in_group = slice(first - group_start, first - group_start + width)
                    h_minus = work.tile([H, width], BF16, name="h_minus")
                    nc.scalar.activation(h_minus[:], z[:, in_group], ACT.Relu, scale=-SLOPE)
                    y = banks.tile([H, width], F32, name="y", tag="bank")
                    nc.tensor.matmul(y[:], w_hid_sb[:], h_plus[:, in_group], start=True, stop=False)
                    nc.tensor.matmul(y[:], w_hid_minus[:], h_minus[:], start=False, stop=True)
                    products[t, first] = y

            def second_layer(t, first, width):
                y = products[t, first]
                low = work.tile([H, width], F32, name="low")
                if (t, first) == (1, 0):
                    nc.vector.tensor_scalar(low[:], y[:], SLOPE, b_hid_low[:, 0:1], op0=MULT, op1=ADD)
                else:
                    nc.scalar.activation(low[:], y[:], ACT.Identity, bias=b_hid_low[:, 0:1], scale=SLOPE)
                result = results.tile([H, width], F32, name="result")
                nc.vector.scalar_tensor_tensor(
                    out=result[:], in0=y[:], scalar=b_hid_col[:, 0:1], in1=low[:], op0=ADD, op1=MAX
                )
                nc.sync.dma_start(out[:, t * N + first : t * N + first + width], result[:])

            for step in range(len(groups) + LAG):
                if step < len(groups):
                    for t, first, width in groups[step]:
                        piece_ahead = t * PIECES + first // PIECE + AHEAD
                        if first % PIECE == 0 and piece_ahead < len(pieces):
                            spread(*pieces[piece_ahead])
                    first_layer(groups[step])
                if step >= LAG:
                    for chunk in groups[step - LAG]:
                        second_layer(*chunk)
